import numpy as np
import ml_dtypes


def mxq(x, axis, fmt="e4m3"):
    dtype, down = {"e4m3": (ml_dtypes.float8_e4m3fn, 7), "e5m2": (ml_dtypes.float8_e5m2, 14)}[fmt]
    v = np.moveaxis(np.asarray(x, np.float32).astype(ml_dtypes.bfloat16).astype(np.float64), axis, -1)
    blocks = v.reshape(v.shape[:-1] + (-1, 32))
    amax = np.abs(blocks).max(-1, keepdims=True)
    byte = np.maximum(np.where(amax > 0, np.frexp(amax)[1] - 1 + 127, 0) - down, 1)
    scale = np.exp2(byte - 127.0)
    codes = (blocks / scale).astype(np.float32).astype(dtype).astype(np.float64)
    return np.moveaxis((codes * scale).reshape(v.shape), -1, axis)


WIDE = False


def mx_kscale(k):
    if not WIDE:
        return np.ones(k)
    levels = np.array([10, -10, 5, -5, 0])
    if k % 512:
        return np.exp2(np.random.permutation(np.resize(levels, k // 32))).repeat(32)
    a = np.empty((k // 512, 16))
    for p in range(k // 512):
        a[p, :8] = np.random.permutation(np.resize(levels, 8))
        for g in range(8):
            far = levels[np.abs(levels - a[p, g]) >= 10]
            a[p, g + 8] = far[np.random.randint(len(far))]
    return np.exp2(a.ravel()).repeat(32)


BF16 = ml_dtypes.bfloat16


def bf(x):
    return np.asarray(x, np.float32).astype(BF16)


def f64(x):
    return np.asarray(x).astype(np.float64)


B, N, C = 64, 16, 512
NEG_SLOPE = 0.2


def leaky(v):
    return np.where(v >= 0, v, NEG_SLOPE * v)


def setup_inputs():
    s, t = mx_kscale(C), mx_kscale(C)
    w1 = np.random.standard_normal((2, C, C)) * 0.7 / np.sqrt(C) / s[None, :, None] * t
    return {"F": bf(np.random.standard_normal((B, N, C)) * s),
            "W1": bf(w1.reshape(2 * C, C)),
            "b1": bf(np.random.standard_normal(C) * 0.2 * t),
            "W2": bf(np.random.standard_normal((C, C)) / np.sqrt(C) / t[:, None]),
            "b2": bf(np.random.standard_normal(C) * 0.2)}


def reference(F, W1, b1, W2, b2):
    Fq = mxq(f64(F), 2, "e4m3")
    W1 = f64(W1)
    A = Fq @ mxq(W1[:C], 0, "e4m3")
    Bp = Fq @ mxq(W1[C:], 0, "e4m3")
    h = leaky(A[:, :, None, :] + Bp[:, None, :, :] + f64(b1))
    h = leaky((mxq(h, 3, "e4m3") @ mxq(f64(W2), 0, "e4m3")) + f64(b2))
    return h.sum(-2)

@@ -1,0 +1,333 @@
+from contextlib import ExitStack
+
+import concourse.mybir as mybir
+from concourse.masks import make_identity
+
+FLOPS = 2 * 1024 * 1024 * 512 + 2 * 16384 * 512 * 512
+
+F32 = mybir.dt.float32
+BF16 = mybir.dt.bfloat16
+U32 = mybir.dt.uint32
+U8 = mybir.dt.uint8
+FP8X4 = mybir.dt.float8_e4m3fn_x4
+ALU = mybir.AluOpType
+ACT = mybir.ActivationFunctionType
+
+P = 128
+SETS = 64
+NODES = 16
+C = 512
+PACK = 4
+CHUNKS = C // P
+WIN = 8
+COLS = WIN * SETS
+TILES = 2 * NODES
+HALF = COLS // 2
+SLOPE = 0.2
+
+AHEAD = 4
+VS = 96
+V_BANKS = 3
+X_BANKS = 2
+LATE = [(0, 4), (5, 9), (10, 14), (15, 15)]
+
+
+def tile_nonlocalmp_pa_t_kernel(tc, F, W1, b1, W2, b2, out):
+    nc = tc.nc
+    with ExitStack() as ctx:
+        ctx.enter_context(tc.manual_schedule())
+        const = ctx.enter_context(tc.tile_pool(name="const", bufs=1))
+        work = ctx.enter_context(tc.tile_pool(name="work", bufs=2))
+        psum = ctx.enter_context(tc.psum_pool(name="psum", bufs=X_BANKS))
+
+        b1r = const.tile([P, CHUNKS], BF16, name="b1r", tag="b1r")
+        b2r = const.tile([P, CHUNKS], BF16, name="b2r", tag="b2r")
+        nc.scalar.dma_start(out=b1r[:], in_=b1.rearrange("(p t) -> p t", t=CHUNKS))
+        nc.scalar.dma_start(out=b2r[:], in_=b2.rearrange("(p t) -> p t", t=CHUNKS))
+
+        w1_raw = const.tile([P, 2, PACK, C], BF16, name="w1_raw", tag="w1_raw")
+        for a in range(2):
+            nc.sync.dma_start(
+                out=w1_raw[:, a], in_=W1[a * C : (a + 1) * C, :].rearrange("(p t) c -> p t c", t=PACK)
+            )
+        f_raw = const.tile([P, 8, C], BF16, name="f_raw", tag="f_raw")
+        f_rows = F.rearrange("b i c -> (b i) c").rearrange("(g p) c -> p g c", p=P)
+        nc.sync.dma_start(out=f_raw[:, 0:4, :], in_=f_rows[:, 0:4, :])
+        nc.sync.dma_start(out=f_raw[:, 4:8, :], in_=f_rows[:, 4:8, :])
+        w2_raw = const.tile([P, PACK, C], BF16, name="w2_raw", tag="w2_raw")
+        nc.sync.dma_start(out=w2_raw[:], in_=W2.rearrange("(p t) n -> p t n", t=PACK))
+
+        ident = const.tile([P, P], F32, name="ident", tag="ident")
+        make_identity(nc, ident[:])
+
+        f_grp = const.tile([P, NODES, SETS, 2], F32, name="f_grp", tag="f_grp", align_bytes=64)
+        fc = const.tile([P, 2 * NODES * SETS], U32, name="fc", tag="fc", align_bytes=64)
+        fs = const.tile([P, 2 * NODES * SETS], U8, name="fs", tag="fs", align_bytes=64)
+        for gg in range(4):
+            xt = psum.tile([P, 2, 2, P], F32, name="xt", tag="v", bufs=V_BANKS)
+            for gp in range(2):
+                words = f_raw[:, 2 * gg + gp, :].bitcast(F32)
+                for u in range(2):
+                    nc.tensor.transpose(
+                        out=xt[:, u, gp, :], in_=words[:, u : 2 * P : 2], identity=ident[:]
+                    )
+            nc.scalar.copy(
+                out=f_grp[:, :, 16 * gg : 16 * gg + 16, :],
+                in_=xt[:].rearrange("p u g (b i) -> p i (g b) u", i=NODES),
+            )
+
+        w1_grp = const.tile([P, 2, CHUNKS, P, PACK], BF16, name="w1_grp", tag="w1_grp", align_bytes=64)
+        w1c = const.tile([P, 2 * C], U32, name="w1c", tag="w1c", align_bytes=64)
+        w1s = const.tile([P, 2 * C], U8, name="w1s", tag="w1s", align_bytes=64)
+        w2_grp = const.tile([P, CHUNKS, P, PACK], BF16, name="w2_grp", tag="w2_grp", align_bytes=64)
+        w2c = const.tile([P, C], U32, name="w2c", tag="w2c", align_bytes=64)
+        w2s = const.tile([P, C], U8, name="w2s", tag="w2s", align_bytes=64)
+        for a in range(2):
+            nc.vector.tensor_copy(
+                out=w1_grp[:, a].rearrange("p o m t -> p m t o"),
+                in_=w1_raw[:, a].rearrange("p t (m o) -> p m t o", o=CHUNKS),
+            )
+        for a in range(2):
+            nc.vector.quantize_mx(
+                out=w1c[:, a * C : (a + 1) * C].bitcast(FP8X4),
+                scales=w1s[:, a * C : (a + 1) * C],
+                in_=w1_grp[:, a].rearrange("p o m t -> p (o m t)"),
+            )
+
+        b1f = const.tile([P, CHUNKS], F32, name="b1f", tag="b1f")
+        nb2 = const.tile([P, CHUNKS], F32, name="nb2", tag="nb2")
+        b2x = const.tile([P, CHUNKS], F32, name="b2x", tag="b2x")
+        nc.vector.tensor_copy(out=b1f[:], in_=b1r[:])
+        nc.vector.tensor_scalar(out=nb2[:], in0=b2r[:], scalar1=-1.0, scalar2=None, op0=ALU.mult)
+        nc.vector.tensor_scalar(out=b2x[:], in0=b2r[:], scalar1=20.0, scalar2=None, op0=ALU.mult)
+        b1s = const.tile([P, CHUNKS], F32, name="b1s", tag="b1s")
+        nc.vector.tensor_scalar(out=b1s[:], in0=b1r[:], scalar1=SLOPE, scalar2=None, op0=ALU.mult)
+
+        f_bf = f_grp[:].rearrange("p i b u -> p (i b u)").bitcast(BF16)
+        for hf in range(2):
+            nc.vector.quantize_mx(
+                out=fc[:, hf * COLS : (hf + 1) * COLS].bitcast(FP8X4),
+                scales=fs[:, hf * COLS : (hf + 1) * COLS],
+                in_=f_bf[:, hf * COLS * PACK : (hf + 1) * COLS * PACK],
+            )
+
+        acc = [
+            [const.tile([P, COLS], F32, name="acc%d%d" % (h, m), tag="acc%d%d" % (h, m)) for m in range(CHUNKS)]
+            for h in range(2)
+        ]
+
+        pq_tiles = {}
+        hid_tiles = {}
+        code_tiles = {}
+        lin = {}
+
+        def mx_pass(dst, lw, ls, rw, rs, start, stop):
+            nc.tensor.matmul_mx(
+                out=dst,
+                lhsT=lw.bitcast(FP8X4),
+                lhsT_scale=ls,
+                rhs=rw.bitcast(FP8X4),
+                rhs_scale=rs,
+                start=start,
+                stop=stop,
+            )
+
+        def pair_sums(n, t):
+            if n >= TILES:
+                return
+            if t == 0:
+                pq_tiles[n] = work.tile([P, 2, CHUNKS, COLS], BF16, name="pre", tag="pre", bufs=AHEAD + 1)
+            first_node = WIN * (n // NODES)
+            a0 = SETS * first_node
+            b0 = SETS * (first_node + n % NODES)
+            vt = psum.tile([P, COLS], F32, name="vt", tag="v", bufs=V_BANKS)
+            wa = slice(t * P, (t + 1) * P)
+            wb = slice(C + t * P, C + (t + 1) * P)
+            mx_pass(vt[:], w1c[:, wa], w1s[:, wa], fc[:, a0 : a0 + COLS], fs[:, a0 : a0 + COLS], True, False)
+            mx_pass(vt[:], w1c[:, wb], w1s[:, wb], fc[:, b0 : b0 + COLS], fs[:, b0 : b0 + COLS], False, True)
+            p_out = pq_tiles[n][:, 0, t, :]
+            q_out = pq_tiles[n][:, 1, t, :]
+            if n < 2 and t % 2 == 1:
+                nc.vector.tensor_scalar(out=p_out, in0=vt[:], scalar1=b1f[:, t : t + 1], scalar2=None, op0=ALU.add)
+                nc.vector.tensor_scalar(
+                    out=q_out, in0=vt[:], scalar1=b1f[:, t : t + 1], scalar2=SLOPE, op0=ALU.add, op1=ALU.mult
+                )
+            else:
+                nc.scalar.activation(out=p_out, in_=vt[:], func=ACT.Identity, bias=b1f[:, t : t + 1], scale=1.0)
+                nc.scalar.activation(out=q_out, in_=vt[:], func=ACT.Identity, bias=b1s[:, t : t + 1], scale=SLOPE)
+
+        def leaky_max(n):
+            if n >= TILES:
+                return
+            pq = pq_tiles[n]
+            nc.vector.tensor_tensor(out=pq[:, 0], in0=pq[:, 0], in1=pq[:, 1], op=ALU.max)
+
+        def regroup_gpsimd(n, part):
+            if n >= TILES:
+                return
+            if part == 0:
+                ht = work.tile([P, HALF, PACK], BF16, name="hida", tag="hida", bufs=3, align_bytes=64)
+            else:
+                ht = work.tile([P, HALF, PACK], BF16, name="hidb", tag="hidb", bufs=1, align_bytes=64)
+            hid_tiles[(n, part)] = ht
+            lo = part * HALF + VS
+            hi = (part + 1) * HALF
+            nc.gpsimd.tensor_scalar(
+                out=ht[:, VS:HALF, :],
+                in0=pq_tiles[n][:, 0, :, lo:hi].rearrange("p t w -> p w t"),
+                scalar1=1.0,
+                scalar2=0.0,
+                op0=ALU.mult,
+                op1=ALU.add,
+            )
+
+        def regroup_vector(n, part):
+            if n >= TILES:
+                return
+            lo = part * HALF
+            nc.vector.tensor_copy(
+                out=hid_tiles[(n, part)][:, 0:VS, :].rearrange("p (c i) t -> p c t i", i=4),
+                in_=pq_tiles[n][:, 0, :, lo : lo + VS].rearrange("p t (c i) -> p c t i", i=4),
+            )
+
+        def quantise_hidden(n):
+            if n >= TILES or n < 0:
+                return
+            hc = const.tile([P, COLS], U32, name="hc%d" % n, tag="hc%d" % n, align_bytes=64)
+            hs = const.tile([P, COLS], U8, name="hs%d" % n, tag="hs%d" % n, align_bytes=64)
+            code_tiles[n] = (hc, hs)
+            for part in (1, 0):
+                cols = slice(part * HALF, (part + 1) * HALF)
+                nc.vector.quantize_mx(
+                    out=hc[:, cols].bitcast(FP8X4),
+                    scales=hs[:, cols],
+                    in_=hid_tiles[(n, part)][:].rearrange("p w t -> p (w t)"),
+                )
+
+        def second_matmul(n, m):
+            hc, hs = code_tiles[n]
+            xs = psum.tile([P, COLS], F32, name="xs", tag="x")
+            wm = slice(m * P, (m + 1) * P)
+            mx_pass(xs[:], w2c[:, wm], w2s[:, wm], hc[:], hs[:], True, True)
+            return xs
+
+        def linear_pass(n, m, tag, bufs):
+            hc, hs = code_tiles[n]
+            s = n % NODES
+            if s == 0:
+                lin[m] = psum.tile([P, COLS], F32, name="lin%d" % m, tag=tag, bufs=bufs)
+            wm = slice(m * P, (m + 1) * P)
+            mx_pass(lin[m][:], w2c[:, wm], w2s[:, wm], hc[:], hs[:], s == 0, s == NODES - 1)
+
+        def linear_now(n, m):
+            linear_pass(n, m, "lin%d" % m, 1)
+
+        def linear_late(h, first, last):
+            for s in range(first, last + 1):
+                linear_pass(NODES * h + s, CHUNKS - 1, "v", V_BANKS)
+
+        def relu_sum(n, m, xs):
+            a = acc[n // NODES][m]
+            if n % NODES == 0:
+                nc.vector.tensor_scalar(
+                    out=a[:], in0=xs[:], scalar1=nb2[:, m : m + 1], scalar2=b2x[:, m : m + 1],
+                    op0=ALU.max, op1=ALU.add,
+                )
+            else:
+                nc.vector.scalar_tensor_tensor(
+                    out=a[:], in0=xs[:], scalar=nb2[:, m : m + 1], in1=a[:], op0=ALU.max, op1=ALU.add
+                )
+
+        def join_sums(h, m):
+            nc.vector.scalar_tensor_tensor(
+                out=acc[h][m][:], in0=lin[m][:], scalar=0.25, in1=acc[h][m][:], op0=ALU.mult, op1=ALU.add
+            )
+
+        def transpose_block(tp, h, m, q):
+            nc.tensor.transpose(out=tp[:, m, :], in_=acc[h][m][:, q * P : (q + 1) * P], identity=ident[:])
+
+        def store_block(tp, h, q, on_vector, second_queue):
+            res = work.tile([P, P, CHUNKS], F32, name="res", tag="res", bufs=4)
+            src = tp[:].rearrange("p m c -> p c m")
+            if on_vector:
+                nc.vector.tensor_scalar(out=res[:], in0=src, scalar1=0.8, scalar2=None, op0=ALU.mult)
+            else:
+                nc.scalar.mul(out=res[:], in_=src, mul=0.8)
+            queues = [nc.sync, second_queue]
+            for k in range(2):
+                queues[k].dma_start(
+                    out=out[:, WIN * h + 2 * q + k, :],
+                    in_=res[k * SETS : (k + 1) * SETS].rearrange("p c m -> p (c m)"),
+                )
+
+        for t in range(CHUNKS):
+            pair_sums(0, t)
+        nc.vector.tensor_copy(
+            out=w2_grp[:].rearrange("p o m t -> p m t o"),
+            in_=w2_raw[:].rearrange("p t (m o) -> p m t o", o=CHUNKS),
+        )
+        for t in range(CHUNKS):
+            pair_sums(1, t)
+        nc.vector.quantize_mx(
+            out=w2c[:].bitcast(FP8X4), scales=w2s[:], in_=w2_grp[:].rearrange("p o m t -> p (o m t)")
+        )
+
+        leaky_max(0)
+        for n in range(-2, TILES):
+            live = n >= 0
+            regroup_gpsimd(n + 2, 0)
+            if live:
+                x0 = second_matmul(n, 0)
+                x1 = second_matmul(n, 1)
+            pair_sums(n + AHEAD, 0)
+            if live:
+                relu_sum(n, 0, x0)
+                linear_now(n, 0)
+                x2 = second_matmul(n, 2)
+                relu_sum(n, 1, x1)
+            regroup_vector(n + 2, 0)
+            if n == -2:
+                nc.vector.quantize_mx(out=fc[:, 1024:2048].bitcast(FP8X4), scales=fs[:, 1024:2048], in_=f_bf)
+            quantise_hidden(n + 1)
+            regroup_gpsimd(n + 2, 1)
+            pair_sums(n + AHEAD, 1)
+            if live:
+                x3 = second_matmul(n, 3)
+                relu_sum(n, 2, x2)
+                linear_now(n, 1)
+            pair_sums(n + AHEAD, 2)
+            if live:
+                linear_now(n, 2)
+            if NODES <= n < NODES + 8:
+                linear_late(0, 2 * (n - NODES), 2 * (n - NODES) + 1)
+            if n >= TILES - 4:
+                linear_late(1, LATE[n - TILES + 4][0], LATE[n - TILES + 4][1])
+            pair_sums(n + AHEAD, 3)
+            if live:
+                relu_sum(n, 3, x3)
+            leaky_max(n + 3)
+            regroup_vector(n + 2, 1)
+            if n == NODES - 1:
+                for m in range(CHUNKS - 1):
+                    join_sums(0, m)
+            if n == NODES + 7:
+                join_sums(0, CHUNKS - 1)
+            if NODES + 8 <= n < NODES + 12:
+                q = n - NODES - 8
+                tp = psum.tile([P, CHUNKS, P], F32, name="tp", tag="v", bufs=V_BANKS)
+                for m in range(CHUNKS):
+                    transpose_block(tp, 0, m, q)
+                store_block(tp, 0, q, False, nc.sync)
+
+        tps = []
+        for q in range(4):
+            if q < 2:
+                tps.append(psum.tile([P, CHUNKS, P], F32, name="tq%d" % q, tag="v", bufs=V_BANKS))
+            else:
+                tps.append(psum.tile([P, CHUNKS, P], F32, name="tq%d" % q, tag="x", bufs=X_BANKS))
+        for m in range(CHUNKS):
+            join_sums(1, m)
+            for q in range(4):
+                transpose_block(tps[q], 1, m, q)
+        for q in range(4):
+            store_block(tps[q], 1, q, q % 2 == 1, nc.scalar)

@@ -24,12 +24,9 @@ COLS = WIN * SETS
 TILES = 2 * NODES
 HALF = COLS // 2
 SLOPE = 0.2
-
-AHEAD = 4
-VS = 96
 V_BANKS = 3
 X_BANKS = 2
-LATE = [(0, 4), (5, 9), (10, 14), (15, 15)]
+LATE = {16: (0, 0, 3), 17: (0, 4, 7), 18: (0, 8, 11), 19: (0, 12, 15), 29: (1, 0, 7), 30: (1, 8, 11), 31: (1, 12, 15)}
 
 
 def tile_nonlocalmp_pa_t_kernel(tc, F, W1, b1, W2, b2, out):
@@ -45,16 +42,21 @@ def tile_nonlocalmp_pa_t_kernel(tc, F, W1, b1, W2, b2, out):
         nc.scalar.dma_start(out=b1r[:], in_=b1.rearrange("(p t) -> p t", t=CHUNKS))
         nc.scalar.dma_start(out=b2r[:], in_=b2.rearrange("(p t) -> p t", t=CHUNKS))
 
+        f_raw = const.tile([P, 2, 4, C], BF16, name="f_raw", tag="f_raw")
         w1_raw = const.tile([P, 2, PACK, C], BF16, name="w1_raw", tag="w1_raw")
+
+        def load_f(h):
+            for e in range(2):
+                n0 = WIN * h + 4 * e
+                nc.sync.dma_start(out=f_raw[e * SETS : (e + 1) * SETS, h], in_=F[:, n0 : n0 + 4, :])
+
+        load_f(0)
         for a in range(2):
             nc.sync.dma_start(
                 out=w1_raw[:, a], in_=W1[a * C : (a + 1) * C, :].rearrange("(p t) c -> p t c", t=PACK)
             )
-        f_raw = const.tile([P, 8, C], BF16, name="f_raw", tag="f_raw")
-        f_rows = F.rearrange("b i c -> (b i) c").rearrange("(g p) c -> p g c", p=P)
-        nc.sync.dma_start(out=f_raw[:, 0:4, :], in_=f_rows[:, 0:4, :])
-        nc.sync.dma_start(out=f_raw[:, 4:8, :], in_=f_rows[:, 4:8, :])
         w2_raw = const.tile([P, PACK, C], BF16, name="w2_raw", tag="w2_raw")
+        load_f(1)
         nc.sync.dma_start(out=w2_raw[:], in_=W2.rearrange("(p t) n -> p t n", t=PACK))
 
         ident = const.tile([P, P], F32, name="ident", tag="ident")
@@ -63,17 +65,27 @@ def tile_nonlocalmp_pa_t_kernel(tc, F, W1, b1, W2, b2, out):
         f_grp = const.tile([P, NODES, SETS, 2], F32, name="f_grp", tag="f_grp", align_bytes=64)
         fc = const.tile([P, 2 * NODES * SETS], U32, name="fc", tag="fc", align_bytes=64)
         fs = const.tile([P, 2 * NODES * SETS], U8, name="fs", tag="fs", align_bytes=64)
-        for gg in range(4):
-            xt = psum.tile([P, 2, 2, P], F32, name="xt", tag="v", bufs=V_BANKS)
-            for gp in range(2):
-                words = f_raw[:, 2 * gg + gp, :].bitcast(F32)
-                for u in range(2):
-                    nc.tensor.transpose(
-                        out=xt[:, u, gp, :], in_=words[:, u : 2 * P : 2], identity=ident[:]
-                    )
-            nc.scalar.copy(
-                out=f_grp[:, :, 16 * gg : 16 * gg + 16, :],
-                in_=xt[:].rearrange("p u g (b i) -> p i (g b) u", i=NODES),
+        f_bf = f_grp[:].rearrange("p i b u -> p (i b u)").bitcast(BF16)
+
+        def transpose_f(h):
+            for rr in range(2):
+                xt = psum.tile([P, 2, 2, P], F32, name="xt", tag="v", bufs=V_BANKS)
+                for r in range(2):
+                    words = f_raw[:, h, 2 * rr + r, :].bitcast(F32)
+                    for u in range(2):
+                        nc.tensor.transpose(out=xt[:, u, r, :], in_=words[:, u : 2 * P : 2], identity=ident[:])
+                p0 = WIN * h + 4 * rr
+                nc.scalar.copy(
+                    out=f_grp[:, p0 : p0 + 4].rearrange("p i b u -> p (i b) u"),
+                    in_=xt[:].rearrange("p u r c -> p (r c) u"),
+                )
+
+        def quantise_f(h, copy):
+            c0 = copy * NODES * SETS + h * COLS
+            nc.vector.quantize_mx(
+                out=fc[:, c0 : c0 + COLS].bitcast(FP8X4),
+                scales=fs[:, c0 : c0 + COLS],
+                in_=f_bf[:, h * COLS * PACK : (h + 1) * COLS * PACK],
             )
 
         w1_grp = const.tile([P, 2, CHUNKS, P, PACK], BF16, name="w1_grp", tag="w1_grp", align_bytes=64)
@@ -82,134 +94,155 @@ def tile_nonlocalmp_pa_t_kernel(tc, F, W1, b1, W2, b2, out):
         w2_grp = const.tile([P, CHUNKS, P, PACK], BF16, name="w2_grp", tag="w2_grp", align_bytes=64)
         w2c = const.tile([P, C], U32, name="w2c", tag="w2c", align_bytes=64)
         w2s = const.tile([P, C], U8, name="w2s", tag="w2s", align_bytes=64)
-        for a in range(2):
-            nc.vector.tensor_copy(
-                out=w1_grp[:, a].rearrange("p o m t -> p m t o"),
-                in_=w1_raw[:, a].rearrange("p t (m o) -> p m t o", o=CHUNKS),
-            )
-        for a in range(2):
+
+        def quantise_w1(a):
             nc.vector.quantize_mx(
                 out=w1c[:, a * C : (a + 1) * C].bitcast(FP8X4),
                 scales=w1s[:, a * C : (a + 1) * C],
                 in_=w1_grp[:, a].rearrange("p o m t -> p (o m t)"),
             )
 
+        def sort_w1(copy, a, m0, m1):
+            copy(
+                out=w1_grp[:, a, :, m0:m1, :].rearrange("p o m t -> p m t o"),
+                in_=w1_raw[:, a, :, CHUNKS * m0 : CHUNKS * m1].rearrange("p t (m o) -> p m t o", o=CHUNKS),
+            )
+
+        transpose_f(0)
+        sort_w1(nc.vector.tensor_copy, 0, 0, P)
+        quantise_f(0, 0)
+        quantise_w1(0)
+        sort_w1(nc.vector.tensor_copy, 1, 0, P // 2)
+        sort_w1(nc.scalar.copy, 1, P // 2, P)
+        quantise_w1(1)
+
         b1f = const.tile([P, CHUNKS], F32, name="b1f", tag="b1f")
         nb2 = const.tile([P, CHUNKS], F32, name="nb2", tag="nb2")
         b2x = const.tile([P, CHUNKS], F32, name="b2x", tag="b2x")
-        nc.vector.tensor_copy(out=b1f[:], in_=b1r[:])
-        nc.vector.tensor_scalar(out=nb2[:], in0=b2r[:], scalar1=-1.0, scalar2=None, op0=ALU.mult)
-        nc.vector.tensor_scalar(out=b2x[:], in0=b2r[:], scalar1=20.0, scalar2=None, op0=ALU.mult)
         b1s = const.tile([P, CHUNKS], F32, name="b1s", tag="b1s")
-        nc.vector.tensor_scalar(out=b1s[:], in0=b1r[:], scalar1=SLOPE, scalar2=None, op0=ALU.mult)
-
-        f_bf = f_grp[:].rearrange("p i b u -> p (i b u)").bitcast(BF16)
-        for hf in range(2):
-            nc.vector.quantize_mx(
-                out=fc[:, hf * COLS : (hf + 1) * COLS].bitcast(FP8X4),
-                scales=fs[:, hf * COLS : (hf + 1) * COLS],
-                in_=f_bf[:, hf * COLS * PACK : (hf + 1) * COLS * PACK],
-            )
+        nc.gpsimd.tensor_scalar(out=b1f[:], in0=b1r[:], scalar1=1.0, scalar2=0.0, op0=ALU.mult, op1=ALU.add)
+        nc.gpsimd.tensor_scalar(out=b1s[:], in0=b1r[:], scalar1=SLOPE, scalar2=0.0, op0=ALU.mult, op1=ALU.add)
+        nc.gpsimd.tensor_scalar(out=nb2[:], in0=b2r[:], scalar1=-1.0, scalar2=0.0, op0=ALU.mult, op1=ALU.add)
+        nc.gpsimd.tensor_scalar(out=b2x[:], in0=b2r[:], scalar1=20.0, scalar2=0.0, op0=ALU.mult, op1=ALU.add)
 
         acc = [
             [const.tile([P, COLS], F32, name="acc%d%d" % (h, m), tag="acc%d%d" % (h, m)) for m in range(CHUNKS)]
             for h in range(2)
         ]
-
         pq_tiles = {}
         hid_tiles = {}
         code_tiles = {}
         lin = {}
+        banks = {}
 
         def mx_pass(dst, lw, ls, rw, rs, start, stop):
             nc.tensor.matmul_mx(
-                out=dst,
-                lhsT=lw.bitcast(FP8X4),
-                lhsT_scale=ls,
-                rhs=rw.bitcast(FP8X4),
-                rhs_scale=rs,
-                start=start,
-                stop=stop,
+                out=dst, lhsT=lw.bitcast(FP8X4), lhsT_scale=ls, rhs=rw.bitcast(FP8X4), rhs_scale=rs,
+                start=start, stop=stop,
             )
 
-        def pair_sums(n, t):
+        def pair_first(n, t):
             if n >= TILES:
                 return
             if t == 0:
-                pq_tiles[n] = work.tile([P, 2, CHUNKS, COLS], BF16, name="pre", tag="pre", bufs=AHEAD + 1)
-            first_node = WIN * (n // NODES)
-            a0 = SETS * first_node
-            b0 = SETS * (first_node + n % NODES)
+                pq_tiles[n] = work.tile([P, 2, CHUNKS, COLS], BF16, name="pre", tag="pre", bufs=4)
+            a0 = SETS * WIN * (n // NODES)
             vt = psum.tile([P, COLS], F32, name="vt", tag="v", bufs=V_BANKS)
+            banks[(n, t)] = vt
             wa = slice(t * P, (t + 1) * P)
-            wb = slice(C + t * P, C + (t + 1) * P)
             mx_pass(vt[:], w1c[:, wa], w1s[:, wa], fc[:, a0 : a0 + COLS], fs[:, a0 : a0 + COLS], True, False)
+
+        def pair_second(n, t, fused):
+            if n >= TILES:
+                return
+            vt = banks[(n, t)]
+            b0 = SETS * (WIN * (n // NODES) + n % NODES)
+            wb = slice(C + t * P, C + (t + 1) * P)
             mx_pass(vt[:], w1c[:, wb], w1s[:, wb], fc[:, b0 : b0 + COLS], fs[:, b0 : b0 + COLS], False, True)
             p_out = pq_tiles[n][:, 0, t, :]
             q_out = pq_tiles[n][:, 1, t, :]
-            if n < 2 and t % 2 == 1:
-                nc.vector.tensor_scalar(out=p_out, in0=vt[:], scalar1=b1f[:, t : t + 1], scalar2=None, op0=ALU.add)
-                nc.vector.tensor_scalar(
-                    out=q_out, in0=vt[:], scalar1=b1f[:, t : t + 1], scalar2=SLOPE, op0=ALU.add, op1=ALU.mult
-                )
-            else:
+            nc.scalar.activation(out=q_out, in_=vt[:], func=ACT.Identity, bias=b1s[:, t : t + 1], scale=SLOPE)
+            if not fused:
                 nc.scalar.activation(out=p_out, in_=vt[:], func=ACT.Identity, bias=b1f[:, t : t + 1], scale=1.0)
-                nc.scalar.activation(out=q_out, in_=vt[:], func=ACT.Identity, bias=b1s[:, t : t + 1], scale=SLOPE)
 
-        def leaky_max(n):
+        def pair_sums(n, t, fused):
+            pair_first(n, t)
+            pair_second(n, t, fused)
+
+        def leaky_bank(n, t):
             if n >= TILES:
                 return
             pq = pq_tiles[n]
-            nc.vector.tensor_tensor(out=pq[:, 0], in0=pq[:, 0], in1=pq[:, 1], op=ALU.max)
+            nc.vector.scalar_tensor_tensor(
+                out=pq[:, 0, t, :], in0=banks[(n, t)][:], scalar=b1f[:, t : t + 1], in1=pq[:, 1, t, :],
+                op0=ALU.add, op1=ALU.max,
+            )
+
+        def leaky_max(n, first, last):
+            if n >= TILES:
+                return
+            pq = pq_tiles[n]
+            nc.vector.tensor_tensor(
+                out=pq[:, 0, first : last + 1], in0=pq[:, 0, first : last + 1], in1=pq[:, 1, first : last + 1],
+                op=ALU.max,
+            )
+
+        def scalar_columns(n):
+            return 192 if n >= TILES - 2 else 64
 
         def regroup_gpsimd(n, part):
             if n >= TILES:
                 return
-            if part == 0:
-                ht = work.tile([P, HALF, PACK], BF16, name="hida", tag="hida", bufs=3, align_bytes=64)
-            else:
-                ht = work.tile([P, HALF, PACK], BF16, name="hidb", tag="hidb", bufs=1, align_bytes=64)
+            ht = work.tile([P, HALF, PACK], BF16, name="hid%d" % part, tag="hid%d" % part, bufs=2, align_bytes=64)
             hid_tiles[(n, part)] = ht
-            lo = part * HALF + VS
-            hi = (part + 1) * HALF
+            last = HALF - scalar_columns(n) * part
             nc.gpsimd.tensor_scalar(
-                out=ht[:, VS:HALF, :],
-                in0=pq_tiles[n][:, 0, :, lo:hi].rearrange("p t w -> p w t"),
-                scalar1=1.0,
-                scalar2=0.0,
-                op0=ALU.mult,
-                op1=ALU.add,
+                out=ht[:, 0:last],
+                in0=pq_tiles[n][:, 0, :, part * HALF : part * HALF + last].rearrange("p t w -> p w t"),
+                scalar1=1.0, scalar2=0.0, op0=ALU.mult, op1=ALU.add,
+            )
+
+        def regroup_scalar(n):
+            if n >= TILES:
+                return
+            sc = scalar_columns(n)
+            nc.scalar.copy(
+                out=hid_tiles[(n, 1)][:, HALF - sc : HALF].rearrange("p (c i) t -> p c t i", i=4),
+                in_=pq_tiles[n][:, 0, :, COLS - sc : COLS].rearrange("p t (c i) -> p c t i", i=4),
             )
 
         def regroup_vector(n, part):
-            if n >= TILES:
-                return
-            lo = part * HALF
+            ht = work.tile([P, HALF, PACK], BF16, name="hid%d" % part, tag="hid%d" % part, bufs=2, align_bytes=64)
+            hid_tiles[(n, part)] = ht
             nc.vector.tensor_copy(
-                out=hid_tiles[(n, part)][:, 0:VS, :].rearrange("p (c i) t -> p c t i", i=4),
-                in_=pq_tiles[n][:, 0, :, lo : lo + VS].rearrange("p t (c i) -> p c t i", i=4),
+                out=ht[:].rearrange("p (c i) t -> p c t i", i=4),
+                in_=pq_tiles[n][:, 0, :, part * HALF : (part + 1) * HALF].rearrange("p t (c i) -> p c t i", i=4),
             )
 
-        def quantise_hidden(n):
-            if n >= TILES or n < 0:
+        def quantise_hidden(n, part):
+            if n >= TILES:
                 return
-            hc = const.tile([P, COLS], U32, name="hc%d" % n, tag="hc%d" % n, align_bytes=64)
-            hs = const.tile([P, COLS], U8, name="hs%d" % n, tag="hs%d" % n, align_bytes=64)
-            code_tiles[n] = (hc, hs)
-            for part in (1, 0):
-                cols = slice(part * HALF, (part + 1) * HALF)
-                nc.vector.quantize_mx(
-                    out=hc[:, cols].bitcast(FP8X4),
-                    scales=hs[:, cols],
-                    in_=hid_tiles[(n, part)][:].rearrange("p w t -> p (w t)"),
-                )
+            if part == 0:
+                hc = const.tile([P, COLS], U32, name="hc%d" % n, tag="hc%d" % n, align_bytes=64)
+                hs = const.tile([P, COLS], U8, name="hs%d" % n, tag="hs%d" % n, align_bytes=64)
+                code_tiles[n] = (hc, hs)
+            hc, hs = code_tiles[n]
+            cols = slice(part * HALF, (part + 1) * HALF)
+            nc.vector.quantize_mx(
+                out=hc[:, cols].bitcast(FP8X4), scales=hs[:, cols],
+                in_=hid_tiles[(n, part)][:].rearrange("p w t -> p (w t)"),
+            )
+
+        xb = {}
 
         def second_matmul(n, m):
+            if n >= TILES:
+                return
             hc, hs = code_tiles[n]
             xs = psum.tile([P, COLS], F32, name="xs", tag="x")
             wm = slice(m * P, (m + 1) * P)
             mx_pass(xs[:], w2c[:, wm], w2s[:, wm], hc[:], hs[:], True, True)
-            return xs
+            xb[(n, m)] = xs
 
         def linear_pass(n, m, tag, bufs):
             hc, hs = code_tiles[n]
@@ -222,12 +255,9 @@ def tile_nonlocalmp_pa_t_kernel(tc, F, W1, b1, W2, b2, out):
         def linear_now(n, m):
             linear_pass(n, m, "lin%d" % m, 1)
 
-        def linear_late(h, first, last):
-            for s in range(first, last + 1):
-                linear_pass(NODES * h + s, CHUNKS - 1, "v", V_BANKS)
-
-        def relu_sum(n, m, xs):
+        def relu_sum(n, m):
             a = acc[n // NODES][m]
+            xs = xb[(n, m)]
             if n % NODES == 0:
                 nc.vector.tensor_scalar(
                     out=a[:], in0=xs[:], scalar1=nb2[:, m : m + 1], scalar2=b2x[:, m : m + 1],
@@ -256,78 +286,86 @@ def tile_nonlocalmp_pa_t_kernel(tc, F, W1, b1, W2, b2, out):
             queues = [nc.sync, second_queue]
             for k in range(2):
                 queues[k].dma_start(
-                    out=out[:, WIN * h + 2 * q + k, :],
+                    out=out[:, WIN * h + 4 * k + q, :],
                     in_=res[k * SETS : (k + 1) * SETS].rearrange("p c m -> p (c m)"),
                 )
 
         for t in range(CHUNKS):
-            pair_sums(0, t)
-        nc.vector.tensor_copy(
+            pair_sums(0, t, True)
+            leaky_bank(0, t)
+        nc.gpsimd.tensor_scalar(
             out=w2_grp[:].rearrange("p o m t -> p m t o"),
-            in_=w2_raw[:].rearrange("p t (m o) -> p m t o", o=CHUNKS),
+            in0=w2_raw[:].rearrange("p t (m o) -> p m t o", o=CHUNKS),
+            scalar1=1.0, scalar2=0.0, op0=ALU.mult, op1=ALU.add,
         )
-        for t in range(CHUNKS):
-            pair_sums(1, t)
+        transpose_f(1)
+        quantise_f(1, 0)
+        pair_sums(1, 0, True)
+        regroup_vector(0, 0)
+        regroup_vector(0, 1)
         nc.vector.quantize_mx(
             out=w2c[:].bitcast(FP8X4), scales=w2s[:], in_=w2_grp[:].rearrange("p o m t -> p (o m t)")
         )
+        quantise_hidden(0, 0)
+        quantise_hidden(0, 1)
+        leaky_bank(1, 0)
+        for t in range(1, CHUNKS):
+            pair_sums(1, t, False)
+        second_matmul(0, 0)
+        second_matmul(0, 1)
+        pair_sums(2, 0, True)
+        pair_sums(2, 1, False)
+        leaky_max(1, 1, 3)
 
-        leaky_max(0)
-        for n in range(-2, TILES):
-            live = n >= 0
-            regroup_gpsimd(n + 2, 0)
-            if live:
-                x0 = second_matmul(n, 0)
-                x1 = second_matmul(n, 1)
-            pair_sums(n + AHEAD, 0)
-            if live:
-                relu_sum(n, 0, x0)
-                linear_now(n, 0)
-                x2 = second_matmul(n, 2)
-                relu_sum(n, 1, x1)
-            regroup_vector(n + 2, 0)
-            if n == -2:
-                nc.vector.quantize_mx(out=fc[:, 1024:2048].bitcast(FP8X4), scales=fs[:, 1024:2048], in_=f_bf)
-            quantise_hidden(n + 1)
-            regroup_gpsimd(n + 2, 1)
-            pair_sums(n + AHEAD, 1)
-            if live:
-                x3 = second_matmul(n, 3)
-                relu_sum(n, 2, x2)
-                linear_now(n, 1)
-            pair_sums(n + AHEAD, 2)
-            if live:
-                linear_now(n, 2)
-            if NODES <= n < NODES + 8:
-                linear_late(0, 2 * (n - NODES), 2 * (n - NODES) + 1)
-            if n >= TILES - 4:
-                linear_late(1, LATE[n - TILES + 4][0], LATE[n - TILES + 4][1])
-            pair_sums(n + AHEAD, 3)
-            if live:
-                relu_sum(n, 3, x3)
-            leaky_max(n + 3)
-            regroup_vector(n + 2, 1)
+        for n in range(TILES):
+            regroup_gpsimd(n + 1, 0)
+            regroup_gpsimd(n + 1, 1)
+            regroup_scalar(n + 1)
+            leaky_bank(n + 2, 0)
+            pair_sums(n + 2, 2, False)
+            relu_sum(n, 0)
+            pair_sums(n + 2, 3, False)
+            second_matmul(n, 2)
+            linear_now(n, 0)
+            relu_sum(n, 1)
+            second_matmul(n, 3)
+            relu_sum(n, 2)
+            linear_now(n, 1)
+            relu_sum(n, 3)
+            linear_now(n, 2)
+            quantise_hidden(n + 1, 0)
+            quantise_hidden(n + 1, 1)
+            pair_sums(n + 3, 0, True)
+            pair_sums(n + 3, 1, False)
+            second_matmul(n + 1, 0)
+            second_matmul(n + 1, 1)
+            if n in LATE:
+                h, first, last = LATE[n]
+                for s in range(first, last + 1):
+                    linear_pass(NODES * h + s, CHUNKS - 1, "v", V_BANKS)
+            leaky_max(n + 2, 1, 3)
+            if n == 2:
+                quantise_f(0, 1)
+            if n == 4:
+                quantise_f(1, 1)
             if n == NODES - 1:
                 for m in range(CHUNKS - 1):
                     join_sums(0, m)
-            if n == NODES + 7:
+            if n == 19:
                 join_sums(0, CHUNKS - 1)
-            if NODES + 8 <= n < NODES + 12:
-                q = n - NODES - 8
+            if 20 <= n < 24:
+                q = n - 20
                 tp = psum.tile([P, CHUNKS, P], F32, name="tp", tag="v", bufs=V_BANKS)
                 for m in range(CHUNKS):
                     transpose_block(tp, 0, m, q)
                 store_block(tp, 0, q, False, nc.sync)
 
-        tps = []
         for q in range(4):
-            if q < 2:
-                tps.append(psum.tile([P, CHUNKS, P], F32, name="tq%d" % q, tag="v", bufs=V_BANKS))
-            else:
-                tps.append(psum.tile([P, CHUNKS, P], F32, name="tq%d" % q, tag="x", bufs=X_BANKS))
-        for m in range(CHUNKS):
-            join_sums(1, m)
-            for q in range(4):
-                transpose_block(tps[q], 1, m, q)
-        for q in range(4):
-            store_block(tps[q], 1, q, q % 2 == 1, nc.scalar)
+            tp = psum.tile([P, CHUNKS, P], F32, name="tq%d" % q, tag="v", bufs=V_BANKS)
+            cols = slice(q * P, (q + 1) * P)
+            for m in range(CHUNKS):
+                a = acc[1][m][:, cols]
+                nc.vector.scalar_tensor_tensor(out=a, in0=lin[m][:, cols], scalar=0.25, in1=a, op0=ALU.mult, op1=ALU.add)
+            for m in range(CHUNKS):
+                transpose_block(tp, 1, m, q)
+            store_block(tp, 1, q, False, nc.scalar)

@@ -26,7 +26,7 @@ HALF = COLS // 2
 SLOPE = 0.2
 V_BANKS = 3
 X_BANKS = 2
-LATE = {16: (0, 0, 3), 17: (0, 4, 7), 18: (0, 8, 11), 19: (0, 12, 15), 29: (1, 0, 7), 30: (1, 8, 11), 31: (1, 12, 15)}
+LATE = dict([(n, (0, 1, 1)) for n in range(8, 16)]+[(n, (0, 1, 1)) for n in range(24, 32)])
 
 
 def tile_nonlocalmp_pa_t_kernel(tc, F, W1, b1, W2, b2, out):
@@ -115,6 +115,8 @@ def tile_nonlocalmp_pa_t_kernel(tc, F, W1, b1, W2, b2, out):
         sort_w1(nc.vector.tensor_copy, 1, 0, P // 2)
         sort_w1(nc.scalar.copy, 1, P // 2, P)
         quantise_w1(1)
+        transpose_f(1)
+        quantise_f(1, 0)
 
         b1f = const.tile([P, CHUNKS], F32, name="b1f", tag="b1f")
         nb2 = const.tile([P, CHUNKS], F32, name="nb2", tag="nb2")
@@ -144,7 +146,7 @@ def tile_nonlocalmp_pa_t_kernel(tc, F, W1, b1, W2, b2, out):
         def pair_first(n, t):
             if n >= TILES:
                 return
-            if t == 0:
+            if n not in pq_tiles:
                 pq_tiles[n] = work.tile([P, 2, CHUNKS, COLS], BF16, name="pre", tag="pre", bufs=4)
             a0 = SETS * WIN * (n // NODES)
             vt = psum.tile([P, COLS], F32, name="vt", tag="v", bufs=V_BANKS)
@@ -255,6 +257,14 @@ def tile_nonlocalmp_pa_t_kernel(tc, F, W1, b1, W2, b2, out):
         def linear_now(n, m):
             linear_pass(n, m, "lin%d" % m, 1)
 
+        late_done = [0, 0]
+
+        def late(n, place):
+            for k in range(LATE.get(n, (0, 0, 0))[place]):
+                h = 0 if n < 24 else 1
+                linear_pass(NODES * h + late_done[h], CHUNKS - 1, "v", V_BANKS)
+                late_done[h] += 1
+
         def relu_sum(n, m):
             a = acc[n // NODES][m]
             xs = xb[(n, m)]
@@ -290,17 +300,19 @@ def tile_nonlocalmp_pa_t_kernel(tc, F, W1, b1, W2, b2, out):
                     in_=res[k * SETS : (k + 1) * SETS].rearrange("p c m -> p (c m)"),
                 )
 
+        one = const.tile([P, 1], F32, name="one", tag="one")
+        nc.vector.memset(one[:], 1.0)
+        nc.gpsimd.tensor_scalar(
+            out=w2_grp[:],
+            in0=w2_raw[:].rearrange("p t (m o) -> p o m t", o=CHUNKS),
+            scalar1=one[:], scalar2=0.0, op0=ALU.mult, op1=ALU.add,
+        )
         for t in range(CHUNKS):
             pair_sums(0, t, True)
             leaky_bank(0, t)
-        nc.gpsimd.tensor_scalar(
-            out=w2_grp[:].rearrange("p o m t -> p m t o"),
-            in0=w2_raw[:].rearrange("p t (m o) -> p m t o", o=CHUNKS),
-            scalar1=1.0, scalar2=0.0, op0=ALU.mult, op1=ALU.add,
-        )
-        transpose_f(1)
-        quantise_f(1, 0)
-        pair_sums(1, 0, True)
+        pair_sums(1, 3, True)
+        for t in range(3):
+            pair_sums(1, t, False)
         regroup_vector(0, 0)
         regroup_vector(0, 1)
         nc.vector.quantize_mx(
@@ -308,53 +320,56 @@ def tile_nonlocalmp_pa_t_kernel(tc, F, W1, b1, W2, b2, out):
         )
         quantise_hidden(0, 0)
         quantise_hidden(0, 1)
-        leaky_bank(1, 0)
-        for t in range(1, CHUNKS):
-            pair_sums(1, t, False)
+        leaky_bank(1, 3)
+        pair_sums(2, 3, True)
         second_matmul(0, 0)
         second_matmul(0, 1)
-        pair_sums(2, 0, True)
-        pair_sums(2, 1, False)
-        leaky_max(1, 1, 3)
+        leaky_max(1, 0, 2)
+        regroup_gpsimd(1, 0)
+        regroup_gpsimd(1, 1)
+        for t in range(3):
+            pair_sums(2, t, False)
+            if t == 0:
+                regroup_scalar(1)
+        leaky_bank(2, 3)
 
         for n in range(TILES):
-            regroup_gpsimd(n + 1, 0)
-            regroup_gpsimd(n + 1, 1)
-            regroup_scalar(n + 1)
-            leaky_bank(n + 2, 0)
-            pair_sums(n + 2, 2, False)
             relu_sum(n, 0)
-            pair_sums(n + 2, 3, False)
-            second_matmul(n, 2)
             linear_now(n, 0)
+            pair_sums(n + 3, 3, True)
+            second_matmul(n, 2)
+            late(n, 0)
             relu_sum(n, 1)
+            pair_sums(n + 3, 0, False)
             second_matmul(n, 3)
-            relu_sum(n, 2)
-            linear_now(n, 1)
-            relu_sum(n, 3)
-            linear_now(n, 2)
+            late(n, 1)
             quantise_hidden(n + 1, 0)
             quantise_hidden(n + 1, 1)
-            pair_sums(n + 3, 0, True)
+            linear_now(n, 1)
             pair_sums(n + 3, 1, False)
+            leaky_max(n + 2, 0, 1)
+            leaky_max(n + 2, 2, 2)
+            regroup_gpsimd(n + 2, 0)
+            regroup_gpsimd(n + 2, 1)
+            regroup_scalar(n + 2)
+            relu_sum(n, 2)
+            linear_now(n, 2)
+            relu_sum(n, 3)
             second_matmul(n + 1, 0)
+            pair_first(n + 3, 2)
             second_matmul(n + 1, 1)
-            if n in LATE:
-                h, first, last = LATE[n]
-                for s in range(first, last + 1):
-                    linear_pass(NODES * h + s, CHUNKS - 1, "v", V_BANKS)
-            leaky_max(n + 2, 1, 3)
+            late(n, 2)
+            pair_second(n + 3, 2, False)
+            leaky_bank(n + 3, 3)
             if n == 2:
                 quantise_f(0, 1)
             if n == 4:
                 quantise_f(1, 1)
             if n == NODES - 1:
-                for m in range(CHUNKS - 1):
+                for m in range(CHUNKS):
                     join_sums(0, m)
-            if n == 19:
-                join_sums(0, CHUNKS - 1)
-            if 20 <= n < 24:
-                q = n - 20
+            if 17 <= n < 21:
+                q = n - 17
                 tp = psum.tile([P, CHUNKS, P], F32, name="tp", tag="v", bufs=V_BANKS)
                 for m in range(CHUNKS):
                     transpose_block(tp, 0, m, q)

@@ -26,7 +26,14 @@ HALF = COLS // 2
 SLOPE = 0.2
 V_BANKS = 3
 X_BANKS = 2
-LATE = dict([(n, (0, 1, 1)) for n in range(8, 16)]+[(n, (0, 1, 1)) for n in range(24, 32)])
+JOIN0 = 19
+LATE = dict([(n, (0, 0, 4, 0)) for n in range(16, 20)] + [(29, (1, 2, 0, 2)), (30, (1, 2, 0, 2)), (31, (0, 1, 0, 5))])
+VS = 0
+SS = 64
+YMOD = 1
+XLO = 18
+XHI = 23
+OUT0 = 28
 
 
 def tile_nonlocalmp_pa_t_kernel(tc, F, W1, b1, W2, b2, out):
@@ -63,8 +70,8 @@ def tile_nonlocalmp_pa_t_kernel(tc, F, W1, b1, W2, b2, out):
         make_identity(nc, ident[:])
 
         f_grp = const.tile([P, NODES, SETS, 2], F32, name="f_grp", tag="f_grp", align_bytes=64)
-        fc = const.tile([P, 2 * NODES * SETS], U32, name="fc", tag="fc", align_bytes=64)
-        fs = const.tile([P, 2 * NODES * SETS], U8, name="fs", tag="fs", align_bytes=64)
+        fc = const.tile([P, (NODES + WIN) * SETS], U32, name="fc", tag="fc", align_bytes=64)
+        fs = const.tile([P, (NODES + WIN) * SETS], U8, name="fs", tag="fs", align_bytes=64)
         f_bf = f_grp[:].rearrange("p i b u -> p (i b u)").bitcast(BF16)
 
         def transpose_f(h):
@@ -115,6 +122,7 @@ def tile_nonlocalmp_pa_t_kernel(tc, F, W1, b1, W2, b2, out):
         sort_w1(nc.vector.tensor_copy, 1, 0, P // 2)
         sort_w1(nc.scalar.copy, 1, P // 2, P)
         quantise_w1(1)
+        quantise_f(0, 1)
         transpose_f(1)
         quantise_f(1, 0)
 
@@ -154,25 +162,25 @@ def tile_nonlocalmp_pa_t_kernel(tc, F, W1, b1, W2, b2, out):
             wa = slice(t * P, (t + 1) * P)
             mx_pass(vt[:], w1c[:, wa], w1s[:, wa], fc[:, a0 : a0 + COLS], fs[:, a0 : a0 + COLS], True, False)
 
-        def pair_second(n, t, fused):
+        def pair_second(n, t):
             if n >= TILES:
                 return
             vt = banks[(n, t)]
-            b0 = SETS * (WIN * (n // NODES) + n % NODES)
+            b0 = SETS * ((WIN * (n // NODES) + n % NODES) % NODES)
             wb = slice(C + t * P, C + (t + 1) * P)
             mx_pass(vt[:], w1c[:, wb], w1s[:, wb], fc[:, b0 : b0 + COLS], fs[:, b0 : b0 + COLS], False, True)
             p_out = pq_tiles[n][:, 0, t, :]
             q_out = pq_tiles[n][:, 1, t, :]
             nc.scalar.activation(out=q_out, in_=vt[:], func=ACT.Identity, bias=b1s[:, t : t + 1], scale=SLOPE)
-            if not fused:
+            if not fused(n, t):
                 nc.scalar.activation(out=p_out, in_=vt[:], func=ACT.Identity, bias=b1f[:, t : t + 1], scale=1.0)
 
-        def pair_sums(n, t, fused):
+        def pair_sums(n, t):
             pair_first(n, t)
-            pair_second(n, t, fused)
+            pair_second(n, t)
 
         def leaky_bank(n, t):
-            if n >= TILES:
+            if n >= TILES or not fused(n, t):
                 return
             pq = pq_tiles[n]
             nc.vector.scalar_tensor_tensor(
@@ -183,6 +191,8 @@ def tile_nonlocalmp_pa_t_kernel(tc, F, W1, b1, W2, b2, out):
         def leaky_max(n, first, last):
             if n >= TILES:
                 return
+            if last == 2 and not fused(n, 3):
+                last = 3
             pq = pq_tiles[n]
             nc.vector.tensor_tensor(
                 out=pq[:, 0, first : last + 1], in0=pq[:, 0, first : last + 1], in1=pq[:, 1, first : last + 1],
@@ -190,14 +200,26 @@ def tile_nonlocalmp_pa_t_kernel(tc, F, W1, b1, W2, b2, out):
             )
 
         def scalar_columns(n):
-            return 192 if n >= TILES - 2 else 64
+            return 128 if n >= TILES - 2 else SS
+
+        def fused(n, t):
+            return n == 0 or (t == 3 and n % YMOD == 0 and not XLO <= n < XHI)
+
+        def regroup_share(n):
+            if n >= TILES or VS == 0:
+                return
+            b = HALF - scalar_columns(n)
+            nc.vector.tensor_copy(
+                out=hid_tiles[(n, 1)][:, b - VS : b].rearrange("p (c i) t -> p c t i", i=4),
+                in_=pq_tiles[n][:, 0, :, HALF + b - VS : HALF + b].rearrange("p t (c i) -> p c t i", i=4),
+            )
 
         def regroup_gpsimd(n, part):
             if n >= TILES:
                 return
             ht = work.tile([P, HALF, PACK], BF16, name="hid%d" % part, tag="hid%d" % part, bufs=2, align_bytes=64)
             hid_tiles[(n, part)] = ht
-            last = HALF - scalar_columns(n) * part
+            last = HALF - (scalar_columns(n) + VS) * part
             nc.gpsimd.tensor_scalar(
                 out=ht[:, 0:last],
                 in0=pq_tiles[n][:, 0, :, part * HALF : part * HALF + last].rearrange("p t w -> p w t"),
@@ -208,6 +230,8 @@ def tile_nonlocalmp_pa_t_kernel(tc, F, W1, b1, W2, b2, out):
             if n >= TILES:
                 return
             sc = scalar_columns(n)
+            if sc == 0:
+                return
             nc.scalar.copy(
                 out=hid_tiles[(n, 1)][:, HALF - sc : HALF].rearrange("p (c i) t -> p c t i", i=4),
                 in_=pq_tiles[n][:, 0, :, COLS - sc : COLS].rearrange("p t (c i) -> p c t i", i=4),
@@ -260,8 +284,8 @@ def tile_nonlocalmp_pa_t_kernel(tc, F, W1, b1, W2, b2, out):
         late_done = [0, 0]
 
         def late(n, place):
-            for k in range(LATE.get(n, (0, 0, 0))[place]):
-                h = 0 if n < 24 else 1
+            for k in range(LATE.get(n, (0, 0, 0, 0))[place]):
+                h = 0 if late_done[0] < NODES else 1
                 linear_pass(NODES * h + late_done[h], CHUNKS - 1, "v", V_BANKS)
                 late_done[h] += 1
 
@@ -308,11 +332,11 @@ def tile_nonlocalmp_pa_t_kernel(tc, F, W1, b1, W2, b2, out):
             scalar1=one[:], scalar2=0.0, op0=ALU.mult, op1=ALU.add,
         )
         for t in range(CHUNKS):
-            pair_sums(0, t, True)
+            pair_sums(0, t)
             leaky_bank(0, t)
-        pair_sums(1, 3, True)
+        pair_sums(1, 3)
         for t in range(3):
-            pair_sums(1, t, False)
+            pair_sums(1, t)
         regroup_vector(0, 0)
         regroup_vector(0, 1)
         nc.vector.quantize_mx(
@@ -321,14 +345,14 @@ def tile_nonlocalmp_pa_t_kernel(tc, F, W1, b1, W2, b2, out):
         quantise_hidden(0, 0)
         quantise_hidden(0, 1)
         leaky_bank(1, 3)
-        pair_sums(2, 3, True)
+        pair_sums(2, 3)
         second_matmul(0, 0)
         second_matmul(0, 1)
         leaky_max(1, 0, 2)
         regroup_gpsimd(1, 0)
         regroup_gpsimd(1, 1)
         for t in range(3):
-            pair_sums(2, t, False)
+            pair_sums(2, t)
             if t == 0:
                 regroup_scalar(1)
         leaky_bank(2, 3)
@@ -336,40 +360,40 @@ def tile_nonlocalmp_pa_t_kernel(tc, F, W1, b1, W2, b2, out):
         for n in range(TILES):
             relu_sum(n, 0)
             linear_now(n, 0)
-            pair_sums(n + 3, 3, True)
+            pair_sums(n + 3, 0)
             second_matmul(n, 2)
             late(n, 0)
             relu_sum(n, 1)
-            pair_sums(n + 3, 0, False)
+            linear_now(n, 1)
             second_matmul(n, 3)
             late(n, 1)
+            regroup_share(n + 1)
             quantise_hidden(n + 1, 0)
             quantise_hidden(n + 1, 1)
-            linear_now(n, 1)
-            pair_sums(n + 3, 1, False)
+            pair_sums(n + 3, 3)
+            late(n, 2)
             leaky_max(n + 2, 0, 1)
             leaky_max(n + 2, 2, 2)
             regroup_gpsimd(n + 2, 0)
             regroup_gpsimd(n + 2, 1)
             regroup_scalar(n + 2)
             relu_sum(n, 2)
+            pair_sums(n + 3, 1)
             linear_now(n, 2)
             relu_sum(n, 3)
             second_matmul(n + 1, 0)
             pair_first(n + 3, 2)
             second_matmul(n + 1, 1)
-            late(n, 2)
-            pair_second(n + 3, 2, False)
+            late(n, 3)
+            pair_second(n + 3, 2)
             leaky_bank(n + 3, 3)
-            if n == 2:
-                quantise_f(0, 1)
-            if n == 4:
-                quantise_f(1, 1)
             if n == NODES - 1:
-                for m in range(CHUNKS):
+                for m in range(CHUNKS - 1):
                     join_sums(0, m)
-            if 17 <= n < 21:
-                q = n - 17
+            if n == JOIN0:
+                join_sums(0, CHUNKS - 1)
+            if OUT0 <= n < OUT0 + 4:
+                q = n - OUT0
                 tp = psum.tile([P, CHUNKS, P], F32, name="tp", tag="v", bufs=V_BANKS)
                 for m in range(CHUNKS):
                     transpose_block(tp, 0, m, q)

@@ -27,13 +27,13 @@ SLOPE = 0.2
 V_BANKS = 3
 X_BANKS = 2
 JOIN0 = 19
-LATE = dict([(n, (0, 0, 4, 0)) for n in range(16, 20)] + [(29, (1, 2, 0, 2)), (30, (1, 2, 0, 2)), (31, (0, 1, 0, 5))])
+LATE = dict([(n, (0, 0, 4, 0)) for n in range(16, 20)] + [(29, (2, 2, 0, 2)), (30, (1, 2, 0, 2)), (31, (0, 2, 0, 3))])
 VS = 0
 SS = 64
 YMOD = 1
 XLO = 18
 XHI = 23
-OUT0 = 28
+OUT = {29: (0, 1), 30: (2, 3)}
 
 
 def tile_nonlocalmp_pa_t_kernel(tc, F, W1, b1, W2, b2, out):
@@ -151,13 +151,13 @@ def tile_nonlocalmp_pa_t_kernel(tc, F, W1, b1, W2, b2, out):
                 start=start, stop=stop,
             )
 
-        def pair_first(n, t):
+        def pair_first(n, t, tag="v"):
             if n >= TILES:
                 return
             if n not in pq_tiles:
                 pq_tiles[n] = work.tile([P, 2, CHUNKS, COLS], BF16, name="pre", tag="pre", bufs=4)
             a0 = SETS * WIN * (n // NODES)
-            vt = psum.tile([P, COLS], F32, name="vt", tag="v", bufs=V_BANKS)
+            vt = psum.tile([P, COLS], F32, name="vt", tag=tag, bufs=V_BANKS if tag == "v" else X_BANKS)
             banks[(n, t)] = vt
             wa = slice(t * P, (t + 1) * P)
             mx_pass(vt[:], w1c[:, wa], w1s[:, wa], fc[:, a0 : a0 + COLS], fs[:, a0 : a0 + COLS], True, False)
@@ -175,8 +175,8 @@ def tile_nonlocalmp_pa_t_kernel(tc, F, W1, b1, W2, b2, out):
             if not fused(n, t):
                 nc.scalar.activation(out=p_out, in_=vt[:], func=ACT.Identity, bias=b1f[:, t : t + 1], scale=1.0)
 
-        def pair_sums(n, t):
-            pair_first(n, t)
+        def pair_sums(n, t, tag="v"):
+            pair_first(n, t, tag)
             pair_second(n, t)
 
         def leaky_bank(n, t):
@@ -191,6 +191,8 @@ def tile_nonlocalmp_pa_t_kernel(tc, F, W1, b1, W2, b2, out):
         def leaky_max(n, first, last):
             if n >= TILES:
                 return
+            if n == 1 and last == 2:
+                return
             if last == 2 and not fused(n, 3):
                 last = 3
             pq = pq_tiles[n]
@@ -203,10 +205,12 @@ def tile_nonlocalmp_pa_t_kernel(tc, F, W1, b1, W2, b2, out):
             return 128 if n >= TILES - 2 else SS
 
         def fused(n, t):
-            return n == 0 or (t == 3 and n % YMOD == 0 and not XLO <= n < XHI)
+            return n == 0 or (n == 1 and t == 2) or (t == 3 and n % YMOD == 0 and not XLO <= n < XHI)
 
         def regroup_share(n):
-            if n >= TILES or VS == 0:
+            if n == 1:
+                regroup_vector(1, 1)
+            if n >= TILES or VS == 0 or n == 1:
                 return
             b = HALF - scalar_columns(n)
             nc.vector.tensor_copy(
@@ -332,10 +336,11 @@ def tile_nonlocalmp_pa_t_kernel(tc, F, W1, b1, W2, b2, out):
             scalar1=one[:], scalar2=0.0, op0=ALU.mult, op1=ALU.add,
         )
         for t in range(CHUNKS):
-            pair_sums(0, t)
+            pair_sums(0, t, "v" if t < 3 else "x")
             leaky_bank(0, t)
-        pair_sums(1, 3)
-        for t in range(3):
+        pair_sums(1, 3, "x")
+        pair_sums(1, 2)
+        for t in range(2):
             pair_sums(1, t)
         regroup_vector(0, 0)
         regroup_vector(0, 1)
@@ -345,16 +350,14 @@ def tile_nonlocalmp_pa_t_kernel(tc, F, W1, b1, W2, b2, out):
         quantise_hidden(0, 0)
         quantise_hidden(0, 1)
         leaky_bank(1, 3)
+        leaky_bank(1, 2)
         pair_sums(2, 3)
         second_matmul(0, 0)
         second_matmul(0, 1)
-        leaky_max(1, 0, 2)
+        leaky_max(1, 0, 1)
         regroup_gpsimd(1, 0)
-        regroup_gpsimd(1, 1)
         for t in range(3):
             pair_sums(2, t)
-            if t == 0:
-                regroup_scalar(1)
         leaky_bank(2, 3)
 
         for n in range(TILES):
@@ -376,9 +379,9 @@ def tile_nonlocalmp_pa_t_kernel(tc, F, W1, b1, W2, b2, out):
             leaky_max(n + 2, 2, 2)
             regroup_gpsimd(n + 2, 0)
             regroup_gpsimd(n + 2, 1)
-            regroup_scalar(n + 2)
             relu_sum(n, 2)
             pair_sums(n + 3, 1)
+            regroup_scalar(n + 2)
             linear_now(n, 2)
             relu_sum(n, 3)
             second_matmul(n + 1, 0)
@@ -392,15 +395,17 @@ def tile_nonlocalmp_pa_t_kernel(tc, F, W1, b1, W2, b2, out):
                     join_sums(0, m)
             if n == JOIN0:
                 join_sums(0, CHUNKS - 1)
-            if OUT0 <= n < OUT0 + 4:
-                q = n - OUT0
+            for q in OUT.get(n, ()):
                 tp = psum.tile([P, CHUNKS, P], F32, name="tp", tag="v", bufs=V_BANKS)
                 for m in range(CHUNKS):
                     transpose_block(tp, 0, m, q)
                 store_block(tp, 0, q, False, nc.sync)
 
         for q in range(4):
-            tp = psum.tile([P, CHUNKS, P], F32, name="tq%d" % q, tag="v", bufs=V_BANKS)
+            if q < 2:
+                tp = psum.tile([P, CHUNKS, P], F32, name="tq%d" % q, tag="v", bufs=V_BANKS)
+            else:
+                tp = psum.tile([P, CHUNKS, P], F32, name="tq%d" % q, tag="x", bufs=X_BANKS)
             cols = slice(q * P, (q + 1) * P)
             for m in range(CHUNKS):
                 a = acc[1][m][:, cols]

@@ -27,9 +27,11 @@ SLOPE = 0.2
 V_BANKS = 3
 X_BANKS = 2
 JOIN0 = 19
-LATE = dict([(n, (0, 0, 4, 0)) for n in range(16, 20)] + [(29, (2, 2, 0, 2)), (30, (1, 2, 0, 2)), (31, (0, 2, 0, 3))])
-VS = 0
+LATE = dict([(n, (0, 0, 4, 0)) for n in range(16, 20)] + [(29, (2, 3, 0, 2)), (30, (1, 2, 0, 1)), (31, (5,))])
+VS0 = 0
 SS = 64
+RLO = 99
+RHI = 99
 YMOD = 1
 XLO = 18
 XHI = 23
@@ -49,13 +51,14 @@ def tile_nonlocalmp_pa_t_kernel(tc, F, W1, b1, W2, b2, out):
         nc.scalar.dma_start(out=b1r[:], in_=b1.rearrange("(p t) -> p t", t=CHUNKS))
         nc.scalar.dma_start(out=b2r[:], in_=b2.rearrange("(p t) -> p t", t=CHUNKS))
 
-        f_raw = const.tile([P, 2, 4, C], BF16, name="f_raw", tag="f_raw")
+        f_raw = const.tile([P, 2, 2, 2, C], BF16, name="f_raw", tag="f_raw")
         w1_raw = const.tile([P, 2, PACK, C], BF16, name="w1_raw", tag="w1_raw")
 
+        f_view = F.rearrange("b (q r) c -> (b q) r c", r=4)
+
         def load_f(h):
-            for e in range(2):
-                n0 = WIN * h + 4 * e
-                nc.sync.dma_start(out=f_raw[e * SETS : (e + 1) * SETS, h], in_=F[:, n0 : n0 + 4, :])
+            for g in range(2):
+                nc.sync.dma_start(out=f_raw[:, h, g], in_=f_view[g * P : (g + 1) * P, 2 * h : 2 * h + 2, :])
 
         load_f(0)
         for a in range(2):
@@ -75,17 +78,18 @@ def tile_nonlocalmp_pa_t_kernel(tc, F, W1, b1, W2, b2, out):
         f_bf = f_grp[:].rearrange("p i b u -> p (i b u)").bitcast(BF16)
 
         def transpose_f(h):
-            for rr in range(2):
+            for g in range(2):
                 xt = psum.tile([P, 2, 2, P], F32, name="xt", tag="v", bufs=V_BANKS)
                 for r in range(2):
-                    words = f_raw[:, h, 2 * rr + r, :].bitcast(F32)
+                    words = f_raw[:, h, g, r, :].bitcast(F32)
                     for u in range(2):
-                        nc.tensor.transpose(out=xt[:, u, r, :], in_=words[:, u : 2 * P : 2], identity=ident[:])
-                p0 = WIN * h + 4 * rr
-                nc.scalar.copy(
-                    out=f_grp[:, p0 : p0 + 4].rearrange("p i b u -> p (i b) u"),
-                    in_=xt[:].rearrange("p u r c -> p (r c) u"),
-                )
+                        nc.tensor.transpose(out=xt[:, r, u, :], in_=words[:, u : 2 * P : 2], identity=ident[:])
+                for r in range(2):
+                    p0 = WIN * h + 4 * r
+                    nc.scalar.copy(
+                        out=f_grp[:, p0 : p0 + 4, 32 * g : 32 * g + 32, :],
+                        in_=xt[:, r].rearrange("p u (b q) -> p q b u", q=4),
+                    )
 
         def quantise_f(h, copy):
             c0 = copy * NODES * SETS + h * COLS
@@ -157,7 +161,7 @@ def tile_nonlocalmp_pa_t_kernel(tc, F, W1, b1, W2, b2, out):
             if n not in pq_tiles:
                 pq_tiles[n] = work.tile([P, 2, CHUNKS, COLS], BF16, name="pre", tag="pre", bufs=4)
             a0 = SETS * WIN * (n // NODES)
-            vt = psum.tile([P, COLS], F32, name="vt", tag=tag, bufs=V_BANKS if tag == "v" else X_BANKS)
+            vt = psum.tile([P, COLS], F32, name="vt", tag=tag, bufs=V_BANKS if tag == "v" else 1)
             banks[(n, t)] = vt
             wa = slice(t * P, (t + 1) * P)
             mx_pass(vt[:], w1c[:, wa], w1s[:, wa], fc[:, a0 : a0 + COLS], fs[:, a0 : a0 + COLS], True, False)
@@ -202,7 +206,10 @@ def tile_nonlocalmp_pa_t_kernel(tc, F, W1, b1, W2, b2, out):
             )
 
         def scalar_columns(n):
-            return 128 if n >= TILES - 2 else SS
+            return 128 if n >= TILES - 2 else (SS if not RLO <= n < RHI else 0)
+
+        def vector_columns(n):
+            return VS0 if not RLO <= n < RHI else 64
 
         def fused(n, t):
             return n == 0 or (n == 1 and t == 2) or (t == 3 and n % YMOD == 0 and not XLO <= n < XHI)
@@ -210,9 +217,10 @@ def tile_nonlocalmp_pa_t_kernel(tc, F, W1, b1, W2, b2, out):
         def regroup_share(n):
             if n == 1:
                 regroup_vector(1, 1)
-            if n >= TILES or VS == 0 or n == 1:
+            if n >= TILES or vector_columns(n) == 0 or n == 1:
                 return
             b = HALF - scalar_columns(n)
+            VS = vector_columns(n)
             nc.vector.tensor_copy(
                 out=hid_tiles[(n, 1)][:, b - VS : b].rearrange("p (c i) t -> p c t i", i=4),
                 in_=pq_tiles[n][:, 0, :, HALF + b - VS : HALF + b].rearrange("p t (c i) -> p c t i", i=4),
@@ -223,7 +231,7 @@ def tile_nonlocalmp_pa_t_kernel(tc, F, W1, b1, W2, b2, out):
                 return
             ht = work.tile([P, HALF, PACK], BF16, name="hid%d" % part, tag="hid%d" % part, bufs=2, align_bytes=64)
             hid_tiles[(n, part)] = ht
-            last = HALF - (scalar_columns(n) + VS) * part
+            last = HALF - (scalar_columns(n) + vector_columns(n)) * part
             nc.gpsimd.tensor_scalar(
                 out=ht[:, 0:last],
                 in0=pq_tiles[n][:, 0, :, part * HALF : part * HALF + last].rearrange("p t w -> p w t"),
@@ -323,10 +331,17 @@ def tile_nonlocalmp_pa_t_kernel(tc, F, W1, b1, W2, b2, out):
                 nc.scalar.mul(out=res[:], in_=src, mul=0.8)
             queues = [nc.sync, second_queue]
             for k in range(2):
+                place = WIN * h + 2 * q + k
                 queues[k].dma_start(
-                    out=out[:, WIN * h + 4 * k + q, :],
+                    out=out[:, 4 * (place % 4) + place // 4, :],
                     in_=res[k * SETS : (k + 1) * SETS].rearrange("p c m -> p (c m)"),
                 )
+
+        def store_half0(q):
+            tp = psum.tile([P, CHUNKS, P], F32, name="tp", tag="v", bufs=V_BANKS)
+            for m in range(CHUNKS):
+                transpose_block(tp, 0, m, q)
+            store_block(tp, 0, q, False, nc.sync)
 
         one = const.tile([P, 1], F32, name="one", tag="one")
         nc.vector.memset(one[:], 1.0)
@@ -336,10 +351,10 @@ def tile_nonlocalmp_pa_t_kernel(tc, F, W1, b1, W2, b2, out):
             scalar1=one[:], scalar2=0.0, op0=ALU.mult, op1=ALU.add,
         )
         for t in range(CHUNKS):
-            pair_sums(0, t, "v" if t < 3 else "x")
+            pair_sums(0, t, "v" if t < 3 else "lin0")
             leaky_bank(0, t)
-        pair_sums(1, 3, "x")
-        pair_sums(1, 2)
+        pair_sums(1, 3, "lin1")
+        pair_sums(1, 2, "lin2")
         for t in range(2):
             pair_sums(1, t)
         regroup_vector(0, 0)
@@ -352,15 +367,16 @@ def tile_nonlocalmp_pa_t_kernel(tc, F, W1, b1, W2, b2, out):
         leaky_bank(1, 3)
         leaky_bank(1, 2)
         pair_sums(2, 3)
+        pair_sums(2, 0)
         second_matmul(0, 0)
         second_matmul(0, 1)
         leaky_max(1, 0, 1)
         regroup_gpsimd(1, 0)
-        for t in range(3):
+        for t in range(1, 3):
             pair_sums(2, t)
         leaky_bank(2, 3)
 
-        for n in range(TILES):
+        for n in range(TILES - 1):
             relu_sum(n, 0)
             linear_now(n, 0)
             pair_sums(n + 3, 0)
@@ -387,6 +403,9 @@ def tile_nonlocalmp_pa_t_kernel(tc, F, W1, b1, W2, b2, out):
             second_matmul(n + 1, 0)
             pair_first(n + 3, 2)
             second_matmul(n + 1, 1)
+            if n == TILES - 2:
+                linear_now(n + 1, 0)
+                linear_now(n + 1, 1)
             late(n, 3)
             pair_second(n + 3, 2)
             leaky_bank(n + 3, 3)
@@ -396,20 +415,38 @@ def tile_nonlocalmp_pa_t_kernel(tc, F, W1, b1, W2, b2, out):
             if n == JOIN0:
                 join_sums(0, CHUNKS - 1)
             for q in OUT.get(n, ()):
-                tp = psum.tile([P, CHUNKS, P], F32, name="tp", tag="v", bufs=V_BANKS)
-                for m in range(CHUNKS):
-                    transpose_block(tp, 0, m, q)
-                store_block(tp, 0, q, False, nc.sync)
+                store_half0(q)
 
+        last = TILES - 1
+        relu_sum(last, 0)
+        second_matmul(last, 2)
+        relu_sum(last, 1)
+        second_matmul(last, 3)
+        join_sums(1, 0)
+        join_sums(1, 1)
+        linear_now(last, 2)
+        for q in OUT.get(last, ()):
+            store_half0(q)
+        late(last, 0)
+        relu_sum(last, 2)
+        relu_sum(last, 3)
+        join_sums(1, 2)
+
+        tps = []
         for q in range(4):
             if q < 2:
                 tp = psum.tile([P, CHUNKS, P], F32, name="tq%d" % q, tag="v", bufs=V_BANKS)
             else:
                 tp = psum.tile([P, CHUNKS, P], F32, name="tq%d" % q, tag="x", bufs=X_BANKS)
-            cols = slice(q * P, (q + 1) * P)
-            for m in range(CHUNKS):
-                a = acc[1][m][:, cols]
-                nc.vector.scalar_tensor_tensor(out=a, in0=lin[m][:, cols], scalar=0.25, in1=a, op0=ALU.mult, op1=ALU.add)
-            for m in range(CHUNKS):
+            tps.append(tp)
+            for m in range(CHUNKS - 1):
                 transpose_block(tp, 1, m, q)
-            store_block(tp, 1, q, False, nc.scalar)
+        for q in range(4):
+            cols = slice(q * P, (q + 1) * P)
+            a = acc[1][CHUNKS - 1][:, cols]
+            nc.vector.scalar_tensor_tensor(
+                out=a, in0=lin[CHUNKS - 1][:, cols], scalar=0.25, in1=a, op0=ALU.mult, op1=ALU.add
+            )
+        for q in range(4):
+            transpose_block(tps[q], 1, CHUNKS - 1, q)
+            store_block(tps[q], 1, q, q % 2 == 1, nc.scalar)

@@ -9,6 +9,7 @@ F32 = mybir.dt.float32
 BF16 = mybir.dt.bfloat16
 U32 = mybir.dt.uint32
 U8 = mybir.dt.uint8
+I32 = mybir.dt.int32
 FP8X4 = mybir.dt.float8_e4m3fn_x4
 ALU = mybir.AluOpType
 ACT = mybir.ActivationFunctionType
@@ -30,6 +31,7 @@ JOIN0 = 19
 LATE = dict([(n, (0, 0, 4, 0)) for n in range(16, 20)] + [(29, (2, 3, 0, 2)), (30, (1, 2, 0, 1)), (31, (5,))])
 VS0 = 0
 SS = 64
+WV = 80
 RLO = 99
 RHI = 99
 YMOD = 1
@@ -48,8 +50,6 @@ def tile_nonlocalmp_pa_t_kernel(tc, F, W1, b1, W2, b2, out):
 
         b1r = const.tile([P, CHUNKS], BF16, name="b1r", tag="b1r")
         b2r = const.tile([P, CHUNKS], BF16, name="b2r", tag="b2r")
-        nc.scalar.dma_start(out=b1r[:], in_=b1.rearrange("(p t) -> p t", t=CHUNKS))
-        nc.scalar.dma_start(out=b2r[:], in_=b2.rearrange("(p t) -> p t", t=CHUNKS))
 
         f_raw = const.tile([P, 2, 2, 2, C], BF16, name="f_raw", tag="f_raw")
         w1_raw = const.tile([P, 2, PACK, C], BF16, name="w1_raw", tag="w1_raw")
@@ -60,14 +60,19 @@ def tile_nonlocalmp_pa_t_kernel(tc, F, W1, b1, W2, b2, out):
             for g in range(2):
                 nc.sync.dma_start(out=f_raw[:, h, g], in_=f_view[g * P : (g + 1) * P, 2 * h : 2 * h + 2, :])
 
-        load_f(0)
-        for a in range(2):
+        def load_w1(a):
             nc.sync.dma_start(
                 out=w1_raw[:, a], in_=W1[a * C : (a + 1) * C, :].rearrange("(p t) c -> p t c", t=PACK)
             )
+
+        load_w1(0)
+        load_f(0)
+        load_w1(1)
+        nc.sync.dma_start(out=b1r[:], in_=b1.rearrange("(p t) -> p t", t=CHUNKS))
         w2_raw = const.tile([P, PACK, C], BF16, name="w2_raw", tag="w2_raw")
         load_f(1)
         nc.sync.dma_start(out=w2_raw[:], in_=W2.rearrange("(p t) n -> p t n", t=PACK))
+        nc.sync.dma_start(out=b2r[:], in_=b2.rearrange("(p t) -> p t", t=CHUNKS))
 
         ident = const.tile([P, P], F32, name="ident", tag="ident")
         make_identity(nc, ident[:])
@@ -121,12 +126,13 @@ def tile_nonlocalmp_pa_t_kernel(tc, F, W1, b1, W2, b2, out):
 
         transpose_f(0)
         sort_w1(nc.vector.tensor_copy, 0, 0, P)
-        quantise_f(0, 0)
         quantise_w1(0)
-        sort_w1(nc.vector.tensor_copy, 1, 0, P // 2)
-        sort_w1(nc.scalar.copy, 1, P // 2, P)
+        sort_w1(nc.vector.tensor_copy, 1, 0, WV)
+        sort_w1(nc.scalar.copy, 1, WV, P)
+        quantise_f(0, 0)
         quantise_w1(1)
-        quantise_f(0, 1)
+        nc.sync.dma_start(out=fc[:, 1024:1536].bitcast(I32), in_=fc[:, 0:512].bitcast(I32))
+        nc.sync.dma_start(out=fs[:, 1024:1536].bitcast(I32), in_=fs[:, 0:512].bitcast(I32))
         transpose_f(1)
         quantise_f(1, 0)
 

@@ -30,7 +30,7 @@ X_BANKS = 2
 JOIN0 = 19
 LATE = dict([(n, (0, 0, 4, 0)) for n in range(16, 20)] + [(29, (2, 3, 0, 2)), (30, (1, 2, 0, 1)), (31, (5,))])
 VS0 = 0
-SS = 64
+SS = 80
 WV = 80
 RLO = 99
 RHI = 99
@@ -228,19 +228,23 @@ def tile_nonlocalmp_pa_t_kernel(tc, F, W1, b1, W2, b2, out):
             b = HALF - scalar_columns(n)
             VS = vector_columns(n)
             nc.vector.tensor_copy(
-                out=hid_tiles[(n, 1)][:, b - VS : b].rearrange("p (c i) t -> p c t i", i=4),
+                out=hidden_tile(n)[:, HALF + b - VS : HALF + b].rearrange("p (c i) t -> p c t i", i=4),
                 in_=pq_tiles[n][:, 0, :, HALF + b - VS : HALF + b].rearrange("p t (c i) -> p c t i", i=4),
             )
 
-        def regroup_gpsimd(n, part):
+        def hidden_tile(n):
+            if n not in hid_tiles:
+                hid_tiles[n] = work.tile([P, COLS, PACK], BF16, name="hid", tag="hid", bufs=2, align_bytes=64)
+            return hid_tiles[n]
+
+        def regroup_gpsimd(n):
             if n >= TILES:
                 return
-            ht = work.tile([P, HALF, PACK], BF16, name="hid%d" % part, tag="hid%d" % part, bufs=2, align_bytes=64)
-            hid_tiles[(n, part)] = ht
-            last = HALF - (scalar_columns(n) + vector_columns(n)) * part
+            ht = hidden_tile(n)
+            last = HALF if n == 1 else COLS - scalar_columns(n) - vector_columns(n)
             nc.gpsimd.tensor_scalar(
                 out=ht[:, 0:last],
-                in0=pq_tiles[n][:, 0, :, part * HALF : part * HALF + last].rearrange("p t w -> p w t"),
+                in0=pq_tiles[n][:, 0, :, 0:last].rearrange("p t w -> p w t"),
                 scalar1=1.0, scalar2=0.0, op0=ALU.mult, op1=ALU.add,
             )
 
@@ -251,15 +255,14 @@ def tile_nonlocalmp_pa_t_kernel(tc, F, W1, b1, W2, b2, out):
             if sc == 0:
                 return
             nc.scalar.copy(
-                out=hid_tiles[(n, 1)][:, HALF - sc : HALF].rearrange("p (c i) t -> p c t i", i=4),
+                out=hidden_tile(n)[:, COLS - sc : COLS].rearrange("p (c i) t -> p c t i", i=4),
                 in_=pq_tiles[n][:, 0, :, COLS - sc : COLS].rearrange("p t (c i) -> p c t i", i=4),
             )
 
         def regroup_vector(n, part):
-            ht = work.tile([P, HALF, PACK], BF16, name="hid%d" % part, tag="hid%d" % part, bufs=2, align_bytes=64)
-            hid_tiles[(n, part)] = ht
+            ht = hidden_tile(n)[:, part * HALF : (part + 1) * HALF]
             nc.vector.tensor_copy(
-                out=ht[:].rearrange("p (c i) t -> p c t i", i=4),
+                out=ht.rearrange("p (c i) t -> p c t i", i=4),
                 in_=pq_tiles[n][:, 0, :, part * HALF : (part + 1) * HALF].rearrange("p t (c i) -> p c t i", i=4),
             )
 
@@ -274,7 +277,7 @@ def tile_nonlocalmp_pa_t_kernel(tc, F, W1, b1, W2, b2, out):
             cols = slice(part * HALF, (part + 1) * HALF)
             nc.vector.quantize_mx(
                 out=hc[:, cols].bitcast(FP8X4), scales=hs[:, cols],
-                in_=hid_tiles[(n, part)][:].rearrange("p w t -> p (w t)"),
+                in_=hid_tiles[n][:, cols].rearrange("p w t -> p (w t)"),
             )
 
         xb = {}
@@ -377,7 +380,7 @@ def tile_nonlocalmp_pa_t_kernel(tc, F, W1, b1, W2, b2, out):
         second_matmul(0, 0)
         second_matmul(0, 1)
         leaky_max(1, 0, 1)
-        regroup_gpsimd(1, 0)
+        regroup_gpsimd(1)
         for t in range(1, 3):
             pair_sums(2, t)
         leaky_bank(2, 3)
@@ -399,8 +402,7 @@ def tile_nonlocalmp_pa_t_kernel(tc, F, W1, b1, W2, b2, out):
             late(n, 2)
             leaky_max(n + 2, 0, 1)
             leaky_max(n + 2, 2, 2)
-            regroup_gpsimd(n + 2, 0)
-            regroup_gpsimd(n + 2, 1)
+            regroup_gpsimd(n + 2)
             relu_sum(n, 2)
             pair_sums(n + 3, 1)
             regroup_scalar(n + 2)

@@ -78,8 +78,8 @@ def tile_nonlocalmp_pa_t_kernel(tc, F, W1, b1, W2, b2, out):
         make_identity(nc, ident[:])
 
         f_grp = const.tile([P, NODES, SETS, 2], F32, name="f_grp", tag="f_grp", align_bytes=64)
-        fc = const.tile([P, (NODES + WIN) * SETS], U32, name="fc", tag="fc", align_bytes=64)
-        fs = const.tile([P, (NODES + WIN) * SETS], U8, name="fs", tag="fs", align_bytes=64)
+        fc = const.tile([P, (NODES + WIN) * SETS], U32, name="fc", tag="fc", align_bytes=256)
+        fs = const.tile([P, (NODES + WIN) * SETS], U8, name="fs", tag="fs", align_bytes=256)
         f_bf = f_grp[:].rearrange("p i b u -> p (i b u)").bitcast(BF16)
 
         def transpose_f(h):
@@ -105,11 +105,11 @@ def tile_nonlocalmp_pa_t_kernel(tc, F, W1, b1, W2, b2, out):
             )
 
         w1_grp = const.tile([P, 2, CHUNKS, P, PACK], BF16, name="w1_grp", tag="w1_grp", align_bytes=64)
-        w1c = const.tile([P, 2 * C], U32, name="w1c", tag="w1c", align_bytes=64)
-        w1s = const.tile([P, 2 * C], U8, name="w1s", tag="w1s", align_bytes=64)
+        w1c = const.tile([P, 2 * C], U32, name="w1c", tag="w1c", align_bytes=256)
+        w1s = const.tile([P, 2 * C], U8, name="w1s", tag="w1s", align_bytes=256)
         w2_grp = const.tile([P, CHUNKS, P, PACK], BF16, name="w2_grp", tag="w2_grp", align_bytes=64)
-        w2c = const.tile([P, C], U32, name="w2c", tag="w2c", align_bytes=64)
-        w2s = const.tile([P, C], U8, name="w2s", tag="w2s", align_bytes=64)
+        w2c = const.tile([P, C], U32, name="w2c", tag="w2c", align_bytes=256)
+        w2s = const.tile([P, C], U8, name="w2s", tag="w2s", align_bytes=256)
 
         def quantise_w1(a):
             nc.vector.quantize_mx(
@@ -270,8 +270,8 @@ def tile_nonlocalmp_pa_t_kernel(tc, F, W1, b1, W2, b2, out):
             if n >= TILES:
                 return
             if part == 0:
-                hc = const.tile([P, COLS], U32, name="hc%d" % n, tag="hc%d" % n, align_bytes=64)
-                hs = const.tile([P, COLS], U8, name="hs%d" % n, tag="hs%d" % n, align_bytes=64)
+                hc = const.tile([P, COLS], U32, name="hc%d" % n, tag="hc%d" % n, align_bytes=256)
+                hs = const.tile([P, COLS], U8, name="hs%d" % n, tag="hs%d" % n, align_bytes=256)
                 code_tiles[n] = (hc, hs)
             hc, hs = code_tiles[n]
             cols = slice(part * HALF, (part + 1) * HALF)

from contextlib import ExitStack

import concourse.mybir as mybir
from concourse.masks import make_identity

FLOPS = 2 * 1024 * 1024 * 512 + 2 * 16384 * 512 * 512

F32 = mybir.dt.float32
BF16 = mybir.dt.bfloat16
U32 = mybir.dt.uint32
U8 = mybir.dt.uint8
I32 = mybir.dt.int32
FP8X4 = mybir.dt.float8_e4m3fn_x4
ALU = mybir.AluOpType
ACT = mybir.ActivationFunctionType

P = 128
SETS = 64
NODES = 16
C = 512
PACK = 4
CHUNKS = C // P
WIN = 8
COLS = WIN * SETS
TILES = 2 * NODES
HALF = COLS // 2
SLOPE = 0.2
V_BANKS = 3
X_BANKS = 2
JOIN0 = 19
LATE = dict([(n, (0, 0, 4, 0)) for n in range(16, 20)] + [(29, (2, 3, 0, 2)), (30, (1, 2, 0, 1)), (31, (5,))])
VS0 = 0
SS = 80
WV = 80
RLO = 99
RHI = 99
YMOD = 1
XLO = 18
XHI = 23
OUT = {29: (0, 1), 30: (2, 3)}


def tile_nonlocalmp_pa_t_kernel(tc, F, W1, b1, W2, b2, out):
    nc = tc.nc
    with ExitStack() as ctx:
        ctx.enter_context(tc.manual_schedule())
        const = ctx.enter_context(tc.tile_pool(name="const", bufs=1))
        work = ctx.enter_context(tc.tile_pool(name="work", bufs=2))
        psum = ctx.enter_context(tc.psum_pool(name="psum", bufs=X_BANKS))

        b1r = const.tile([P, CHUNKS], BF16, name="b1r", tag="b1r")
        b2r = const.tile([P, CHUNKS], BF16, name="b2r", tag="b2r")

        f_raw = const.tile([P, 2, 2, 2, C], BF16, name="f_raw", tag="f_raw")
        w1_raw = const.tile([P, 2, PACK, C], BF16, name="w1_raw", tag="w1_raw")

        f_view = F.rearrange("b (q r) c -> (b q) r c", r=4)

        def load_f(h):
            for g in range(2):
                nc.sync.dma_start(out=f_raw[:, h, g], in_=f_view[g * P : (g + 1) * P, 2 * h : 2 * h + 2, :])

        def load_w1(a):
            nc.sync.dma_start(
                out=w1_raw[:, a], in_=W1[a * C : (a + 1) * C, :].rearrange("(p t) c -> p t c", t=PACK)
            )

        load_w1(0)
        load_f(0)
        load_w1(1)
        nc.sync.dma_start(out=b1r[:], in_=b1.rearrange("(p t) -> p t", t=CHUNKS))
        w2_raw = const.tile([P, PACK, C], BF16, name="w2_raw", tag="w2_raw")
        load_f(1)
        nc.sync.dma_start(out=w2_raw[:], in_=W2.rearrange("(p t) n -> p t n", t=PACK))
        nc.sync.dma_start(out=b2r[:], in_=b2.rearrange("(p t) -> p t", t=CHUNKS))

        ident = const.tile([P, P], F32, name="ident", tag="ident")
        make_identity(nc, ident[:])

        f_grp = const.tile([P, NODES, SETS, 2], F32, name="f_grp", tag="f_grp", align_bytes=64)
        fc = const.tile([P, (NODES + WIN) * SETS], U32, name="fc", tag="fc", align_bytes=256)
        fs = const.tile([P, (NODES + WIN) * SETS], U8, name="fs", tag="fs", align_bytes=256)
        f_bf = f_grp[:].rearrange("p i b u -> p (i b u)").bitcast(BF16)

        def transpose_f(h):
            for g in range(2):
                xt = psum.tile([P, 2, 2, P], F32, name="xt", tag="v", bufs=V_BANKS)
                for r in range(2):
                    words = f_raw[:, h, g, r, :].bitcast(F32)
                    for u in range(2):
                        nc.tensor.transpose(out=xt[:, r, u, :], in_=words[:, u : 2 * P : 2], identity=ident[:])
                for r in range(2):
                    p0 = WIN * h + 4 * r
                    nc.scalar.copy(
                        out=f_grp[:, p0 : p0 + 4, 32 * g : 32 * g + 32, :],
                        in_=xt[:, r].rearrange("p u (b q) -> p q b u", q=4),
                    )

        def quantise_f(h, copy):
            c0 = copy * NODES * SETS + h * COLS
            nc.vector.quantize_mx(
                out=fc[:, c0 : c0 + COLS].bitcast(FP8X4),
                scales=fs[:, c0 : c0 + COLS],
                in_=f_bf[:, h * COLS * PACK : (h + 1) * COLS * PACK],
            )

        w1_grp = const.tile([P, 2, CHUNKS, P, PACK], BF16, name="w1_grp", tag="w1_grp", align_bytes=64)
        w1c = const.tile([P, 2 * C], U32, name="w1c", tag="w1c", align_bytes=256)
        w1s = const.tile([P, 2 * C], U8, name="w1s", tag="w1s", align_bytes=256)
        w2_grp = const.tile([P, CHUNKS, P, PACK], BF16, name="w2_grp", tag="w2_grp", align_bytes=64)
        w2c = const.tile([P, C], U32, name="w2c", tag="w2c", align_bytes=256)
        w2s = const.tile([P, C], U8, name="w2s", tag="w2s", align_bytes=256)

        def quantise_w1(a):
            nc.vector.quantize_mx(
                out=w1c[:, a * C : (a + 1) * C].bitcast(FP8X4),
                scales=w1s[:, a * C : (a + 1) * C],
                in_=w1_grp[:, a].rearrange("p o m t -> p (o m t)"),
            )

        def sort_w1(copy, a, m0, m1):
            copy(
                out=w1_grp[:, a, :, m0:m1, :].rearrange("p o m t -> p m t o"),
                in_=w1_raw[:, a, :, CHUNKS * m0 : CHUNKS * m1].rearrange("p t (m o) -> p m t o", o=CHUNKS),
            )

        transpose_f(0)
        sort_w1(nc.vector.tensor_copy, 0, 0, P)
        quantise_w1(0)
        sort_w1(nc.vector.tensor_copy, 1, 0, WV)
        sort_w1(nc.scalar.copy, 1, WV, P)
        quantise_f(0, 0)
        quantise_w1(1)
        nc.sync.dma_start(out=fc[:, 1024:1536].bitcast(I32), in_=fc[:, 0:512].bitcast(I32))
        nc.sync.dma_start(out=fs[:, 1024:1536].bitcast(I32), in_=fs[:, 0:512].bitcast(I32))
        transpose_f(1)
        quantise_f(1, 0)

        b1f = const.tile([P, CHUNKS], F32, name="b1f", tag="b1f")
        nb2 = const.tile([P, CHUNKS], F32, name="nb2", tag="nb2")
        b2x = const.tile([P, CHUNKS], F32, name="b2x", tag="b2x")
        b1s = const.tile([P, CHUNKS], F32, name="b1s", tag="b1s")
        nc.gpsimd.tensor_scalar(out=b1f[:], in0=b1r[:], scalar1=1.0, scalar2=0.0, op0=ALU.mult, op1=ALU.add)
        nc.gpsimd.tensor_scalar(out=b1s[:], in0=b1r[:], scalar1=SLOPE, scalar2=0.0, op0=ALU.mult, op1=ALU.add)
        nc.gpsimd.tensor_scalar(out=nb2[:], in0=b2r[:], scalar1=-1.0, scalar2=0.0, op0=ALU.mult, op1=ALU.add)
        nc.gpsimd.tensor_scalar(out=b2x[:], in0=b2r[:], scalar1=20.0, scalar2=0.0, op0=ALU.mult, op1=ALU.add)

        acc = [
            [const.tile([P, COLS], F32, name="acc%d%d" % (h, m), tag="acc%d%d" % (h, m)) for m in range(CHUNKS)]
            for h in range(2)
        ]
        pq_tiles = {}
        hid_tiles = {}
        code_tiles = {}
        lin = {}
        banks = {}

        def mx_pass(dst, lw, ls, rw, rs, start, stop):
            nc.tensor.matmul_mx(
                out=dst, lhsT=lw.bitcast(FP8X4), lhsT_scale=ls, rhs=rw.bitcast(FP8X4), rhs_scale=rs,
                start=start, stop=stop,
            )

        def pair_first(n, t, tag="v"):
            if n >= TILES:
                return
            if n not in pq_tiles:
                pq_tiles[n] = work.tile([P, 2, CHUNKS, COLS], BF16, name="pre", tag="pre", bufs=4)
            a0 = SETS * WIN * (n // NODES)
            vt = psum.tile([P, COLS], F32, name="vt", tag=tag, bufs=V_BANKS if tag == "v" else 1)
            banks[(n, t)] = vt
            wa = slice(t * P, (t + 1) * P)
            mx_pass(vt[:], w1c[:, wa], w1s[:, wa], fc[:, a0 : a0 + COLS], fs[:, a0 : a0 + COLS], True, False)

        def pair_second(n, t):
            if n >= TILES:
                return
            vt = banks[(n, t)]
            b0 = SETS * ((WIN * (n // NODES) + n % NODES) % NODES)
            wb = slice(C + t * P, C + (t + 1) * P)
            mx_pass(vt[:], w1c[:, wb], w1s[:, wb], fc[:, b0 : b0 + COLS], fs[:, b0 : b0 + COLS], False, True)
            p_out = pq_tiles[n][:, 0, t, :]
            q_out = pq_tiles[n][:, 1, t, :]
            nc.scalar.activation(out=q_out, in_=vt[:], func=ACT.Identity, bias=b1s[:, t : t + 1], scale=SLOPE)
            if not fused(n, t):
                nc.scalar.activation(out=p_out, in_=vt[:], func=ACT.Identity, bias=b1f[:, t : t + 1], scale=1.0)

        def pair_sums(n, t, tag="v"):
            pair_first(n, t, tag)
            pair_second(n, t)

        def leaky_bank(n, t):
            if n >= TILES or not fused(n, t):
                return
            pq = pq_tiles[n]
            nc.vector.scalar_tensor_tensor(
                out=pq[:, 0, t, :], in0=banks[(n, t)][:], scalar=b1f[:, t : t + 1], in1=pq[:, 1, t, :],
                op0=ALU.add, op1=ALU.max,
            )

        def leaky_max(n, first, last):
            if n >= TILES:
                return
            if n == 1 and last == 2:
                return
            if last == 2 and not fused(n, 3):
                last = 3
            pq = pq_tiles[n]
            nc.vector.tensor_tensor(
                out=pq[:, 0, first : last + 1], in0=pq[:, 0, first : last + 1], in1=pq[:, 1, first : last + 1],
                op=ALU.max,
            )

        def scalar_columns(n):
            return 128 if n >= TILES - 2 else (SS if not RLO <= n < RHI else 0)

        def vector_columns(n):
            return VS0 if not RLO <= n < RHI else 64

        def fused(n, t):
            return n == 0 or (n == 1 and t == 2) or (t == 3 and n % YMOD == 0 and not XLO <= n < XHI)

        def regroup_share(n):
            if n == 1:
                regroup_vector(1, 1)
            if n >= TILES or vector_columns(n) == 0 or n == 1:
                return
            b = HALF - scalar_columns(n)
            VS = vector_columns(n)
            nc.vector.tensor_copy(
                out=hidden_tile(n)[:, HALF + b - VS : HALF + b].rearrange("p (c i) t -> p c t i", i=4),
                in_=pq_tiles[n][:, 0, :, HALF + b - VS : HALF + b].rearrange("p t (c i) -> p c t i", i=4),
            )

        def hidden_tile(n):
            if n not in hid_tiles:
                hid_tiles[n] = work.tile([P, COLS, PACK], BF16, name="hid", tag="hid", bufs=2, align_bytes=64)
            return hid_tiles[n]

        def regroup_gpsimd(n):
            if n >= TILES:
                return
            ht = hidden_tile(n)
            last = HALF if n == 1 else COLS - scalar_columns(n) - vector_columns(n)
            nc.gpsimd.tensor_scalar(
                out=ht[:, 0:last],
                in0=pq_tiles[n][:, 0, :, 0:last].rearrange("p t w -> p w t"),
                scalar1=1.0, scalar2=0.0, op0=ALU.mult, op1=ALU.add,
            )

        def regroup_scalar(n):
            if n >= TILES:
                return
            sc = scalar_columns(n)
            if sc == 0:
                return
            nc.scalar.copy(
                out=hidden_tile(n)[:, COLS - sc : COLS].rearrange("p (c i) t -> p c t i", i=4),
                in_=pq_tiles[n][:, 0, :, COLS - sc : COLS].rearrange("p t (c i) -> p c t i", i=4),
            )

        def regroup_vector(n, part):
            ht = hidden_tile(n)[:, part * HALF : (part + 1) * HALF]
            nc.vector.tensor_copy(
                out=ht.rearrange("p (c i) t -> p c t i", i=4),
                in_=pq_tiles[n][:, 0, :, part * HALF : (part + 1) * HALF].rearrange("p t (c i) -> p c t i", i=4),
            )

        def quantise_hidden(n, part):
            if n >= TILES:
                return
            if part == 0:
                hc = const.tile([P, COLS], U32, name="hc%d" % n, tag="hc%d" % n, align_bytes=256)
                hs = const.tile([P, COLS], U8, name="hs%d" % n, tag="hs%d" % n, align_bytes=256)
                code_tiles[n] = (hc, hs)
            hc, hs = code_tiles[n]
            cols = slice(part * HALF, (part + 1) * HALF)
            nc.vector.quantize_mx(
                out=hc[:, cols].bitcast(FP8X4), scales=hs[:, cols],
                in_=hid_tiles[n][:, cols].rearrange("p w t -> p (w t)"),
            )

        xb = {}

        def second_matmul(n, m):
            if n >= TILES:
                return
            hc, hs = code_tiles[n]
            xs = psum.tile([P, COLS], F32, name="xs", tag="x")
            wm = slice(m * P, (m + 1) * P)
            mx_pass(xs[:], w2c[:, wm], w2s[:, wm], hc[:], hs[:], True, True)
            xb[(n, m)] = xs

        def linear_pass(n, m, tag, bufs):
            hc, hs = code_tiles[n]
            s = n % NODES
            if s == 0:
                lin[m] = psum.tile([P, COLS], F32, name="lin%d" % m, tag=tag, bufs=bufs)
            wm = slice(m * P, (m + 1) * P)
            mx_pass(lin[m][:], w2c[:, wm], w2s[:, wm], hc[:], hs[:], s == 0, s == NODES - 1)

        def linear_now(n, m):
            linear_pass(n, m, "lin%d" % m, 1)

        late_done = [0, 0]

        def late(n, place):
            for k in range(LATE.get(n, (0, 0, 0, 0))[place]):
                h = 0 if late_done[0] < NODES else 1
                linear_pass(NODES * h + late_done[h], CHUNKS - 1, "v", V_BANKS)
                late_done[h] += 1

        def relu_sum(n, m):
            a = acc[n // NODES][m]
            xs = xb[(n, m)]
            if n % NODES == 0:
                nc.vector.tensor_scalar(
                    out=a[:], in0=xs[:], scalar1=nb2[:, m : m + 1], scalar2=b2x[:, m : m + 1],
                    op0=ALU.max, op1=ALU.add,
                )
            else:
                nc.vector.scalar_tensor_tensor(
                    out=a[:], in0=xs[:], scalar=nb2[:, m : m + 1], in1=a[:], op0=ALU.max, op1=ALU.add
                )

        def join_sums(h, m):
            nc.vector.scalar_tensor_tensor(
                out=acc[h][m][:], in0=lin[m][:], scalar=0.25, in1=acc[h][m][:], op0=ALU.mult, op1=ALU.add
            )

        def transpose_block(tp, h, m, q):
            nc.tensor.transpose(out=tp[:, m, :], in_=acc[h][m][:, q * P : (q + 1) * P], identity=ident[:])

        def store_block(tp, h, q, on_vector, second_queue):
            res = work.tile([P, P, CHUNKS], F32, name="res", tag="res", bufs=4)
            src = tp[:].rearrange("p m c -> p c m")
            if on_vector:
                nc.vector.tensor_scalar(out=res[:], in0=src, scalar1=0.8, scalar2=None, op0=ALU.mult)
            else:
                nc.scalar.mul(out=res[:], in_=src, mul=0.8)
            queues = [nc.sync, second_queue]
            for k in range(2):
                place = WIN * h + 2 * q + k
                queues[k].dma_start(
                    out=out[:, 4 * (place % 4) + place // 4, :],
                    in_=res[k * SETS : (k + 1) * SETS].rearrange("p c m -> p (c m)"),
                )

        def store_half0(q):
            tp = psum.tile([P, CHUNKS, P], F32, name="tp", tag="v", bufs=V_BANKS)
            for m in range(CHUNKS):
                transpose_block(tp, 0, m, q)
            store_block(tp, 0, q, False, nc.sync)

        one = const.tile([P, 1], F32, name="one", tag="one")
        nc.vector.memset(one[:], 1.0)
        nc.gpsimd.tensor_scalar(
            out=w2_grp[:],
            in0=w2_raw[:].rearrange("p t (m o) -> p o m t", o=CHUNKS),
            scalar1=one[:], scalar2=0.0, op0=ALU.mult, op1=ALU.add,
        )
        for t in range(CHUNKS):
            pair_sums(0, t, "v" if t < 3 else "lin0")
            leaky_bank(0, t)
        pair_sums(1, 3, "lin1")
        pair_sums(1, 2, "lin2")
        for t in range(2):
            pair_sums(1, t)
        regroup_vector(0, 0)
        regroup_vector(0, 1)
        nc.vector.quantize_mx(
            out=w2c[:].bitcast(FP8X4), scales=w2s[:], in_=w2_grp[:].rearrange("p o m t -> p (o m t)")
        )
        quantise_hidden(0, 0)
        quantise_hidden(0, 1)
        leaky_bank(1, 3)
        leaky_bank(1, 2)
        pair_sums(2, 3)
        pair_sums(2, 0)
        second_matmul(0, 0)
        second_matmul(0, 1)
        leaky_max(1, 0, 1)
        regroup_gpsimd(1)
        for t in range(1, 3):
            pair_sums(2, t)
        leaky_bank(2, 3)

        for n in range(TILES - 1):
            relu_sum(n, 0)
            linear_now(n, 0)
            pair_sums(n + 3, 0)
            second_matmul(n, 2)
            late(n, 0)
            relu_sum(n, 1)
            linear_now(n, 1)
            second_matmul(n, 3)
            late(n, 1)
            regroup_share(n + 1)
            quantise_hidden(n + 1, 0)
            quantise_hidden(n + 1, 1)
            pair_sums(n + 3, 3)
            late(n, 2)
            leaky_max(n + 2, 0, 1)
            leaky_max(n + 2, 2, 2)
            regroup_gpsimd(n + 2)
            relu_sum(n, 2)
            pair_sums(n + 3, 1)
            regroup_scalar(n + 2)
            linear_now(n, 2)
            relu_sum(n, 3)
            second_matmul(n + 1, 0)
            pair_first(n + 3, 2)
            second_matmul(n + 1, 1)
            if n == TILES - 2:
                linear_now(n + 1, 0)
                linear_now(n + 1, 1)
            late(n, 3)
            pair_second(n + 3, 2)
            leaky_bank(n + 3, 3)
            if n == NODES - 1:
                for m in range(CHUNKS - 1):
                    join_sums(0, m)
            if n == JOIN0:
                join_sums(0, CHUNKS - 1)
            for q in OUT.get(n, ()):
                store_half0(q)

        last = TILES - 1
        relu_sum(last, 0)
        second_matmul(last, 2)
        relu_sum(last, 1)
        second_matmul(last, 3)
        join_sums(1, 0)
        join_sums(1, 1)
        linear_now(last, 2)
        for q in OUT.get(last, ()):
            store_half0(q)
        late(last, 0)
        relu_sum(last, 2)
        relu_sum(last, 3)
        join_sums(1, 2)

        tps = []
        for q in range(4):
            if q < 2:
                tp = psum.tile([P, CHUNKS, P], F32, name="tq%d" % q, tag="v", bufs=V_BANKS)
            else:
                tp = psum.tile([P, CHUNKS, P], F32, name="tq%d" % q, tag="x", bufs=X_BANKS)
            tps.append(tp)
            for m in range(CHUNKS - 1):
                transpose_block(tp, 1, m, q)
        for q in range(4):
            cols = slice(q * P, (q + 1) * P)
            a = acc[1][CHUNKS - 1][:, cols]
            nc.vector.scalar_tensor_tensor(
                out=a, in0=lin[CHUNKS - 1][:, cols], scalar=0.25, in1=a, op0=ALU.mult, op1=ALU.add
            )
        for q in range(4):
            transpose_block(tps[q], 1, CHUNKS - 1, q)
            store_block(tps[q], 1, q, q % 2 == 1, nc.scalar)
